import numpy as np
import ml_dtypes


def mxq(x, axis, fmt="e4m3"):
    dtype, down = {"e4m3": (ml_dtypes.float8_e4m3fn, 7), "e5m2": (ml_dtypes.float8_e5m2, 14)}[fmt]
    v = np.moveaxis(np.asarray(x, np.float32).astype(ml_dtypes.bfloat16).astype(np.float64), axis, -1)
    blocks = v.reshape(v.shape[:-1] + (-1, 32))
    amax = np.abs(blocks).max(-1, keepdims=True)
    byte = np.maximum(np.where(amax > 0, np.frexp(amax)[1] - 1 + 127, 0) - down, 1)
    scale = np.exp2(byte - 127.0)
    codes = (blocks / scale).astype(np.float32).astype(dtype).astype(np.float64)
    return np.moveaxis((codes * scale).reshape(v.shape), -1, axis)


WIDE = False


def mx_kscale(k):
    if not WIDE:
        return np.ones(k)
    levels = np.array([10, -10, 5, -5, 0])
    a = np.random.permutation(np.resize(levels, k // 512 * 4)).reshape(k // 512, 4)
    idx = np.arange(k)
    return np.exp2(a[idx // 512, idx % 128 // 32])


BF16 = ml_dtypes.bfloat16


def bf(x):
    return np.asarray(x, np.float32).astype(BF16)


def f64(x):
    return np.asarray(x).astype(np.float64)


E2M1 = np.array([0.0, 0.5, 1.0, 1.5, 2.0, 3.0, 4.0, 6.0, -0.0, -0.5, -1.0, -1.5, -2.0, -3.0, -4.0, -6.0])


def pack_weight(w, fmt):
    k, n = w.shape
    w = f64(bf(w)).reshape(k // 32, 32, n)
    amax = np.abs(w).max(1)
    if fmt == "e4m3":
        byte = np.frexp(amax)[1] - 1 + 127 - 7
    else:
        mant, ex = np.frexp(amax / 6.0)
        byte = np.where(mant > 0.5, ex, ex - 1) + 127
    byte = np.clip(np.where(amax > 0, byte, 1), 1, 254)
    scaled = (w * np.exp2(127.0 - byte)[:, None, :]).reshape(k, n).astype(np.float32)
    by_word = np.ascontiguousarray(scaled.reshape(k // 512, 128, 4, n).transpose(0, 1, 3, 2))
    if fmt == "e4m3":
        words = by_word.astype(ml_dtypes.float8_e4m3fn).view(np.uint8)
    else:
        c = by_word.astype(ml_dtypes.float4_e2m1fn).view(np.uint8) & 0xF
        words = c[..., 0::2] | (c[..., 1::2] << 4)
    return np.ascontiguousarray(words), np.ascontiguousarray(byte.astype(np.uint8).reshape(k // 512, 16, n))


def unpack_weight(words, scales, fmt):
    g, p, n, _ = words.shape
    if fmt == "e4m3":
        vals = np.ascontiguousarray(words).view(ml_dtypes.float8_e4m3fn).astype(np.float64)
    else:
        nib = np.empty((g, p, n, 4), np.uint8)
        nib[..., 0::2] = words & 0xF
        nib[..., 1::2] = words >> 4
        vals = E2M1[nib]
    vals = vals * np.repeat(np.exp2(scales.astype(np.float64) - 127.0), 8, axis=1)[..., None]
    return vals.transpose(0, 1, 3, 2).reshape(g * 512, n)


B, T, C, CO, HS, DW, DA, DV, DG = 2, 128, 8192, 1024, 64, 128, 128, 128, 256
H = C // HS
EPS_GN = 0.00064


def setup_inputs():
    n = np.random.standard_normal
    t = mx_kscale(C)
    inputs = {
        "y": bf(n((B, T, C)) * 0.1),
        "r": bf(n((B, T, C))),
        "k": bf(n((B, T, C)) * 0.6),
        "v": bf(n((B, T, C)) * 0.8),
        "g_hid": bf(1.0 / (1.0 + np.exp(-n((B, T, DG))))),
        "g2": bf(n((DG, C)) * 2.0 / np.sqrt(DG) * t),
        "r_k": bf(n((H, HS)) * 0.2 - 0.04),
        "ln_g": bf(1.0 + n((C,)) * 0.1),
        "ln_b": bf(n((C,)) * 0.1),
    }
    w_o = n((CO, C)) * 0.7 / np.sqrt(C) / t
    words, scales = pack_weight(np.ascontiguousarray(w_o.T), "e4m3")
    inputs["W_o_words"] = words
    inputs["W_o_scales"] = scales
    return inputs


def reference(y, r, k, v, g_hid, g2, r_k, ln_g, ln_b, W_o_words, W_o_scales):
    yh = f64(y).reshape(B, T, H, HS)
    mu = np.mean(yh, axis=-1, keepdims=True)
    var = np.mean((yh - mu) ** 2, axis=-1, keepdims=True)
    yn = ((yh - mu) / np.sqrt(var + EPS_GN)).reshape(B, T, C)
    yn = yn * f64(ln_g) + f64(ln_b)
    rh = f64(r).reshape(B, T, H, HS)
    kh = f64(k).reshape(B, T, H, HS)
    vh = f64(v).reshape(B, T, H, HS)
    dot = np.sum(rh * kh * f64(r_k), axis=-1, keepdims=True)
    y2 = yn + (dot * vh).reshape(B, T, C)
    g = f64(g_hid) @ f64(g2)
    z = y2 * g
    return mxq(z, 2, "e4m3") @ unpack_weight(W_o_words, W_o_scales, "e4m3")

@@ -1,0 +1,409 @@
+from contextlib import ExitStack
+
+import concourse.mybir as mybir
+from concourse.masks import make_identity
+
+F32 = mybir.dt.float32
+BF16 = mybir.dt.bfloat16
+I32 = mybir.dt.int32
+U32 = mybir.dt.uint32
+U8 = mybir.dt.uint8
+FP8X4 = mybir.dt.float8_e4m3fn_x4
+ALU = mybir.AluOpType
+ACT = mybir.ActivationFunctionType
+AX = mybir.AxisListType
+
+P = 128
+SEQS = 2
+C = 8192
+CO = 1024
+HEAD = 64
+DG = 256
+EPS = 0.00064
+PACK = 4
+PASS = P * PACK
+PASSES = C // PASS
+PASS_HEADS = PASS // HEAD
+HEAD_PARTS = HEAD // PACK
+SLAB_PASSES = 4
+SLAB = SLAB_PASSES * PASS
+SLABS = C // SLAB
+SLAB_HEADS = SLAB // HEAD
+BLOCK_HEADS = P // HEAD
+BANK_BLOCKS = 4
+N_TILE = 512
+HALVES = CO // N_TILE
+KD = DG // P
+STEPS = SEQS * PASSES
+
+FLOPS = 2 * SEQS * P * C * CO + 2 * SEQS * P * DG * C
+
+
+def tile_full_tmix_params_pc_k_kernel(
+    tc, y, r, k, v, g_hid, g2, r_k, ln_g, ln_b, W_o_words, W_o_scales, out
+):
+    nc = tc.nc
+    with ExitStack() as ctx:
+        const = ctx.enter_context(tc.tile_pool(name="const", bufs=1))
+        loads = ctx.enter_context(tc.tile_pool(name="loads", bufs=2))
+        stats = ctx.enter_context(tc.tile_pool(name="stats", bufs=2))
+        work = ctx.enter_context(tc.tile_pool(name="work", bufs=2))
+        ps_acc = ctx.enter_context(tc.psum_pool(name="ps_acc", bufs=1))
+        ps_a = ctx.enter_context(tc.psum_pool(name="ps_a", bufs=2))
+        ps_one = ctx.enter_context(tc.psum_pool(name="ps_one", bufs=1))
+        ctx.enter_context(tc.manual_schedule())
+
+        ident_f = const.tile([P, P], F32, name="ident_f")
+        make_identity(nc, ident_f[:])
+        ident_b = const.tile([P, P], BF16, name="ident_b")
+        make_identity(nc, ident_b[:])
+
+        planes = const.tile([P, SLABS, CO], U8, name="planes", align_bytes=64)
+        nc.vector.memset(planes[:].bitcast(I32), 0)
+
+        gam_raw = const.tile([P, PASSES, PACK], BF16, name="gam_raw")
+        bet_raw = const.tile([P, PASSES, PACK], BF16, name="bet_raw")
+        nc.scalar.dma_start(out=gam_raw[:], in_=ln_g.rearrange("(g p t) -> p g t", p=P, t=PACK))
+        nc.scalar.dma_start(out=bet_raw[:], in_=ln_b.rearrange("(g p t) -> p g t", p=P, t=PACK))
+        gam = const.tile([P, PASSES * PACK], F32, name="gam")
+        bet = const.tile([P, PASSES * PACK], F32, name="bet")
+        nc.vector.tensor_copy(out=gam[:], in_=gam_raw[:].rearrange("p g t -> p (g t)"))
+        nc.vector.tensor_copy(out=bet[:], in_=bet_raw[:].rearrange("p g t -> p (g t)"))
+
+        rk_rows = const.tile([P, P], BF16, name="rk_rows")
+        nc.vector.memset(rk_rows[:], 0.0)
+        nc.scalar.dma_start(
+            out=rk_rows[0 : C // P, :], in_=r_k.rearrange("(j i) c -> j (i c)", i=BLOCK_HEADS)
+        )
+        rk_cols = ps_one.tile([P, P], BF16, name="rk_cols", tag="blocks")
+        nc.tensor.transpose(rk_cols[:], rk_rows[:], ident_b[:])
+        head_w = const.tile([P, C // P, BLOCK_HEADS], F32, name="head_w")
+        nc.vector.memset(head_w[:], 0.0)
+        for i in range(BLOCK_HEADS):
+            rows = slice(HEAD * i, HEAD * (i + 1))
+            nc.vector.tensor_copy(out=head_w[rows, :, i], in_=rk_cols[rows, 0 : C // P])
+
+        gh = const.tile([P, SEQS, DG], BF16, name="gh")
+        nc.scalar.dma_start(out=gh[:], in_=g_hid.rearrange("b n d -> n b d"))
+        gh_ps = ps_one.tile([P, KD, SEQS, P], BF16, name="gh_ps", tag="blocks")
+        for kd in range(KD):
+            for b in range(SEQS):
+                nc.tensor.transpose(gh_ps[:, kd, b, :], gh[:, b, P * kd : P * (kd + 1)], ident_b[:])
+        gh_t = const.tile([P, KD, SEQS, P], BF16, name="gh_t")
+        nc.vector.tensor_copy(out=gh_t[:], in_=gh_ps[:])
+
+        w_words = [
+            const.tile([P, SLAB_PASSES, CO], U32, name="w_words%d" % s, align_bytes=64)
+            for s in range(SLABS)
+        ]
+        g2_sorted = [
+            const.tile([P, KD, SLAB_PASSES, PACK, P], BF16, name="g2_sorted%d" % s)
+            for s in range(SLABS)
+        ]
+
+        y_of, r_of, k_of, v_of, g2_raw_of = {}, {}, {}, {}, {}
+        bn_of, var_of, both_of, std_of, rstd_of, shift_of = {}, {}, {}, {}, {}, {}
+        words_of, scales_of, acc_of = {}, {}, {}
+        rk_of, rk_ch_of, rk_sb_of, dot_ps_of, dot_of = {}, {}, {}, {}, {}
+        a_tok_of, a_ch_of, yn_of, dv_tok_of, dv_ch_of, y2_of, gate_of = {}, {}, {}, {}, {}, {}, {}
+
+        def slab_cols(u):
+            s = u % SLABS
+            return slice(SLAB * s, SLAB * (s + 1))
+
+        def step_heads(j):
+            o = j % SLAB_PASSES
+            return range(PASS_HEADS * o, PASS_HEADS * (o + 1))
+
+        def by_value(head_cols):
+            return head_cols.rearrange("n (p t) -> n t p", t=PACK)
+
+        def load_y_r_k(u):
+            b = u // SLABS
+            y_of[u] = loads.tile([P, SLAB], BF16, name="y_t", bufs=3)
+            r_of[u] = loads.tile([P, SLAB], BF16, name="r_t")
+            k_of[u] = loads.tile([P, SLAB], BF16, name="k_t")
+            nc.sync.dma_start(out=y_of[u][:], in_=y[b, :, slab_cols(u)])
+            nc.sync.dma_start(out=r_of[u][:], in_=r[b, :, slab_cols(u)])
+            nc.sync.dma_start(out=k_of[u][:], in_=k[b, :, slab_cols(u)])
+
+        def load_v(u):
+            v_of[u] = loads.tile([P, SLAB], BF16, name="v_t")
+            nc.sync.dma_start(out=v_of[u][:], in_=v[u // SLABS, :, slab_cols(u)])
+
+        def load_g2(s):
+            g2_raw_of[s] = loads.tile([P, KD, SLAB], BF16, name="g2_raw")
+            nc.sync.dma_start(
+                out=g2_raw_of[s][:], in_=g2.rearrange("(kd d) c -> d kd c", kd=KD)[:, :, slab_cols(s)]
+            )
+
+        def load_w(s):
+            passes = slice(SLAB_PASSES * s, SLAB_PASSES * (s + 1))
+            for quad in range(4):
+                nc.sync.dma_start(
+                    out=planes[32 * quad : 32 * quad + 16, s, :].bitcast(I32),
+                    in_=W_o_scales[passes, 4 * quad : 4 * quad + 4, :].bitcast(I32),
+                )
+            nc.sync.dma_start(
+                out=w_words[s][:].bitcast(I32),
+                in_=W_o_words[passes].rearrange("g p n t -> p g (n t)").bitcast(I32),
+            )
+
+        def sort_g2(j):
+            s, o = j // SLAB_PASSES, j % SLAB_PASSES
+            for kd in range(KD):
+                nc.gpsimd.tensor_scalar(
+                    out=g2_sorted[s][:, kd, o],
+                    in0=g2_raw_of[s][:, kd, PASS * o : PASS * (o + 1)].rearrange(
+                        "d (p t) -> d t p", t=PACK
+                    ),
+                    scalar1=1.0,
+                    scalar2=0.0,
+                    op0=ALU.mult,
+                    op1=ALU.add,
+                )
+
+        def r_times_k(j):
+            u, o = j // SLAB_PASSES, j % SLAB_PASSES
+            cols = slice(PASS * o, PASS * (o + 1))
+            rk_of[j] = work.tile([P, PASS], F32, name="rk", bufs=3)
+            nc.gpsimd.tensor_tensor(out=rk_of[j][:], in0=r_of[u][:, cols], in1=k_of[u][:, cols], op=ALU.mult)
+
+        def rk_transpose(j):
+            rk_ch_of[j] = ps_one.tile([P, BANK_BLOCKS, P], F32, name="rk_ch", tag="blocks")
+            for i in range(BANK_BLOCKS):
+                nc.tensor.transpose(rk_ch_of[j][:, i, :], rk_of[j][:, P * i : P * (i + 1)], ident_f[:])
+
+        def rk_copy(j):
+            rk_sb_of[j] = work.tile([P, BANK_BLOCKS, P], F32, name="rk_sb", bufs=3)
+            nc.scalar.copy(out=rk_sb_of[j][:], in_=rk_ch_of[j][:])
+
+        def dot_matmul(j):
+            g = j % PASSES
+            dot_ps_of[j] = ps_one.tile([P, PASS_HEADS], F32, name="dot_ps")
+            for i in range(BANK_BLOCKS):
+                nc.tensor.matmul(
+                    out=dot_ps_of[j][:, BLOCK_HEADS * i : BLOCK_HEADS * (i + 1)],
+                    lhsT=rk_sb_of[j][:, i, :],
+                    rhs=head_w[:, BANK_BLOCKS * g + i, :],
+                    start=True,
+                    stop=True,
+                )
+
+        def dot_copy(j):
+            dot_of[j] = stats.tile([P, PASS_HEADS], F32, name="dot", bufs=3)
+            nc.vector.tensor_copy(out=dot_of[j][:], in_=dot_ps_of[j][:])
+
+        def y_stats(j):
+            u = j // SLAB_PASSES
+            if j % SLAB_PASSES == 0:
+                bn_of[u] = stats.tile([P, SLAB_HEADS, 6], F32, name="bn")
+            for h in step_heads(j):
+                nc.vector.bn_stats(out=bn_of[u][:, h, :], in_=y_of[u][:, HEAD * h : HEAD * (h + 1)])
+
+        def variance(u):
+            bn = bn_of[u]
+            both = stats.tile([P, SLAB_HEADS, 3], F32, name="both")
+            nc.vector.tensor_reduce(
+                out=both[:], in_=bn[:].rearrange("n h (e s) -> n h s e", e=2), axis=AX.X, op=ALU.add
+            )
+            gap = stats.tile([P, SLAB_HEADS], F32, name="gap")
+            nc.vector.tensor_tensor(out=gap[:], in0=bn[:, :, 1], in1=bn[:, :, 4], op=ALU.subtract)
+            gap2 = stats.tile([P, SLAB_HEADS], F32, name="gap2")
+            nc.vector.scalar_tensor_tensor(
+                out=gap2[:], in0=gap[:], scalar=0.25, in1=gap[:], op0=ALU.mult, op1=ALU.mult
+            )
+            within = stats.tile([P, SLAB_HEADS], F32, name="within")
+            nc.vector.tensor_scalar(
+                out=within[:], in0=both[:, :, 2], scalar1=1.0 / HEAD, scalar2=EPS, op0=ALU.mult, op1=ALU.add
+            )
+            var_of[u] = stats.tile([P, SLAB_HEADS], F32, name="var_eps")
+            nc.vector.tensor_tensor(out=var_of[u][:], in0=gap2[:], in1=within[:], op=ALU.add)
+            both_of[u] = both
+
+        def root(u):
+            std_of[u] = stats.tile([P, SLAB_HEADS], F32, name="std")
+            nc.scalar.activation(out=std_of[u][:], in_=var_of[u][:], func=ACT.Sqrt)
+
+        def scale_and_shift(u):
+            rstd_of[u] = stats.tile([P, SLAB_HEADS], F32, name="rstd")
+            nc.vector.reciprocal(out=rstd_of[u][:], in_=std_of[u][:])
+            shift_of[u] = stats.tile([P, SLAB_HEADS], F32, name="shift")
+            nc.vector.scalar_tensor_tensor(
+                out=shift_of[u][:],
+                in0=both_of[u][:, :, 1],
+                scalar=-0.5,
+                in1=rstd_of[u][:],
+                op0=ALU.mult,
+                op1=ALU.mult,
+            )
+
+        def normalise(j):
+            u = j // SLAB_PASSES
+            a_tok_of[j] = work.tile([P, PACK, P], F32, name="a_tok", bufs=3)
+            for hh, h in enumerate(step_heads(j)):
+                nc.scalar.activation(
+                    out=a_tok_of[j][:, :, HEAD_PARTS * hh : HEAD_PARTS * (hh + 1)],
+                    in_=by_value(y_of[u][:, HEAD * h : HEAD * (h + 1)]),
+                    func=ACT.Identity,
+                    scale=rstd_of[u][:, h : h + 1],
+                    bias=shift_of[u][:, h : h + 1],
+                )
+
+        def a_transpose(j):
+            a_ch_of[j] = ps_a.tile([P, PACK, P], F32, name="a_ch")
+            for t in range(PACK):
+                nc.tensor.transpose(a_ch_of[j][:, t, :], a_tok_of[j][:, t, :], ident_f[:])
+
+        def gain_and_bias(j):
+            g = j % PASSES
+            yn_of[j] = work.tile([P, PACK, P], F32, name="yn")
+            for t in range(PACK):
+                col = PACK * g + t
+                nc.scalar.activation(
+                    out=yn_of[j][:, t, :],
+                    in_=a_ch_of[j][:, t, :],
+                    func=ACT.Identity,
+                    scale=gam[:, col : col + 1],
+                    bias=bet[:, col : col + 1],
+                )
+
+        def dot_times_v(j):
+            u = j // SLAB_PASSES
+            dv_tok_of[j] = work.tile([P, PACK, P], F32, name="dv_tok", bufs=3)
+            for hh, h in enumerate(step_heads(j)):
+                nc.scalar.activation(
+                    out=dv_tok_of[j][:, :, HEAD_PARTS * hh : HEAD_PARTS * (hh + 1)],
+                    in_=by_value(v_of[u][:, HEAD * h : HEAD * (h + 1)]),
+                    func=ACT.Copy,
+                    scale=dot_of[j][:, hh : hh + 1],
+                )
+
+        def dv_transpose(j):
+            dv_ch_of[j] = ps_one.tile([P, PACK, P], F32, name="dv_ch")
+            for t in range(PACK):
+                nc.tensor.transpose(dv_ch_of[j][:, t, :], dv_tok_of[j][:, t, :], ident_f[:])
+
+        def gate_matmul(j):
+            b, g = j // PASSES, j % PASSES
+            s, o = g // SLAB_PASSES, g % SLAB_PASSES
+            gate_of[j] = ps_one.tile([P, PACK, P], F32, name="gate")
+            for t in range(PACK):
+                for kd in range(KD):
+                    nc.tensor.matmul(
+                        out=gate_of[j][:, t, :],
+                        lhsT=g2_sorted[s][:, kd, o, t, :],
+                        rhs=gh_t[:, kd, b, :],
+                        start=(kd == 0),
+                        stop=(kd == KD - 1),
+                    )
+
+        def add_bonus(j):
+            y2_of[j] = work.tile([P, PACK, P], F32, name="y2")
+            nc.vector.tensor_tensor(out=y2_of[j][:], in0=yn_of[j][:], in1=dv_ch_of[j][:], op=ALU.add)
+
+        def gated_and_quantised(j):
+            u, o = j // SLAB_PASSES, j % SLAB_PASSES
+            if o == 0:
+                words_of[u] = work.tile([P, SLAB_PASSES, P], U32, name="z_words", align_bytes=64)
+                scales_of[u] = work.tile([P, SLAB_PASSES, P], U8, name="z_scales", align_bytes=64)
+            z_bf = work.tile([P, P, PACK], BF16, name="z_bf", align_bytes=64)
+            nc.vector.tensor_tensor(
+                out=z_bf[:],
+                in0=y2_of[j][:].rearrange("p t n -> p n t"),
+                in1=gate_of[j][:].rearrange("p t n -> p n t"),
+                op=ALU.mult,
+            )
+            nc.vector.quantize_mx(
+                out=words_of[u][:, o, :].bitcast(FP8X4),
+                scales=scales_of[u][:, o, :],
+                in_=z_bf[:].rearrange("p n t -> p (n t)"),
+            )
+
+        def project(u):
+            b, s = u // SLABS, u % SLABS
+            if s == 0:
+                acc_of[b] = [ps_acc.tile([P, N_TILE], F32, name="acc%d" % half) for half in range(HALVES)]
+            for o in range(SLAB_PASSES):
+                g = SLAB_PASSES * s + o
+                for half in range(HALVES):
+                    n_cols = slice(N_TILE * half, N_TILE * (half + 1))
+                    nc.tensor.matmul_mx(
+                        out=acc_of[b][half][:],
+                        lhsT=words_of[u][:, o, :].bitcast(FP8X4),
+                        lhsT_scale=scales_of[u][:, o, :],
+                        rhs=w_words[s][:, o, n_cols].bitcast(FP8X4),
+                        rhs_scale=planes[4 * o : P, s, n_cols],
+                        start=(g == 0),
+                        stop=(g == PASSES - 1),
+                    )
+
+        def store(b):
+            for half in range(HALVES):
+                res = work.tile([P, N_TILE], F32, name="res")
+                nc.scalar.copy(out=res[:], in_=acc_of[b][half][:])
+                nc.sync.dma_start(out=out[b, :, N_TILE * half : N_TILE * (half + 1)], in_=res[:])
+
+        def step_due(tick, lead):
+            j = tick + lead
+            return [j] if 0 <= j < STEPS else []
+
+        def slab_due(tick, lead, slabs):
+            first = tick + lead
+            return [first // SLAB_PASSES] if first % SLAB_PASSES == 0 and 0 <= first < SLAB_PASSES * slabs else []
+
+        for tick in range(-12, STEPS + 5):
+            for u in slab_due(tick, 12, SEQS * SLABS):
+                load_y_r_k(u)
+            for s in slab_due(tick, 8, SLABS):
+                load_g2(s)
+            for u in slab_due(tick, 7, SEQS * SLABS):
+                load_v(u)
+            for s in slab_due(tick, 2, SLABS):
+                load_w(s)
+
+            for j in step_due(tick, 0):
+                add_bonus(j)
+            for j in step_due(tick, 3):
+                dot_copy(j)
+            for u in slab_due(tick, 4, SEQS * SLABS):
+                scale_and_shift(u)
+            for j in step_due(tick, 8):
+                y_stats(j)
+            for u in slab_due(tick, 5, SEQS * SLABS):
+                variance(u)
+            for j in step_due(tick, 0):
+                gated_and_quantised(j)
+
+            for j in step_due(tick, 1):
+                gain_and_bias(j)
+            for b in range(SEQS):
+                if tick == PASSES * (b + 1) + 4:
+                    store(b)
+            for j in step_due(tick, 5):
+                rk_copy(j)
+            for u in slab_due(tick, 5, SEQS * SLABS):
+                root(u)
+            for j in step_due(tick, 3):
+                dot_times_v(j)
+            for j in step_due(tick, 4):
+                normalise(j)
+
+            for j in step_due(tick, 1):
+                dv_transpose(j)
+            for j in step_due(tick, 4):
+                dot_matmul(j)
+            for j in step_due(tick, 2):
+                a_transpose(j)
+            for j in step_due(tick, 1):
+                gate_matmul(j)
+            for j in step_due(tick, 6):
+                rk_transpose(j)
+            for u in slab_due(tick, -6, SEQS * SLABS):
+                project(u)
+
+            for j in step_due(tick, 8):
+                r_times_k(j)
+            for j in step_due(tick, 4):
+                if j < PASSES:
+                    sort_g2(j)

@@ -49,8 +49,7 @@ def tile_full_tmix_params_pc_k_kernel(
         stats = ctx.enter_context(tc.tile_pool(name="stats", bufs=2))
         work = ctx.enter_context(tc.tile_pool(name="work", bufs=2))
         ps_acc = ctx.enter_context(tc.psum_pool(name="ps_acc", bufs=1))
-        ps_a = ctx.enter_context(tc.psum_pool(name="ps_a", bufs=2))
-        ps_one = ctx.enter_context(tc.psum_pool(name="ps_one", bufs=1))
+        ps_work = ctx.enter_context(tc.psum_pool(name="ps_work", bufs=2))
         ctx.enter_context(tc.manual_schedule())
 
         ident_f = const.tile([P, P], F32, name="ident_f")
@@ -61,51 +60,35 @@ def tile_full_tmix_params_pc_k_kernel(
         planes = const.tile([P, SLABS, CO], U8, name="planes", align_bytes=64)
         nc.vector.memset(planes[:].bitcast(I32), 0)
 
-        gam_raw = const.tile([P, PASSES, PACK], BF16, name="gam_raw")
-        bet_raw = const.tile([P, PASSES, PACK], BF16, name="bet_raw")
-        nc.scalar.dma_start(out=gam_raw[:], in_=ln_g.rearrange("(g p t) -> p g t", p=P, t=PACK))
-        nc.scalar.dma_start(out=bet_raw[:], in_=ln_b.rearrange("(g p t) -> p g t", p=P, t=PACK))
-        gam = const.tile([P, PASSES * PACK], F32, name="gam")
-        bet = const.tile([P, PASSES * PACK], F32, name="bet")
-        nc.vector.tensor_copy(out=gam[:], in_=gam_raw[:].rearrange("p g t -> p (g t)"))
-        nc.vector.tensor_copy(out=bet[:], in_=bet_raw[:].rearrange("p g t -> p (g t)"))
-
-        rk_rows = const.tile([P, P], BF16, name="rk_rows")
-        nc.vector.memset(rk_rows[:], 0.0)
-        nc.scalar.dma_start(
-            out=rk_rows[0 : C // P, :], in_=r_k.rearrange("(j i) c -> j (i c)", i=BLOCK_HEADS)
-        )
-        rk_cols = ps_one.tile([P, P], BF16, name="rk_cols", tag="blocks")
-        nc.tensor.transpose(rk_cols[:], rk_rows[:], ident_b[:])
-        head_w = const.tile([P, C // P, BLOCK_HEADS], F32, name="head_w")
-        nc.vector.memset(head_w[:], 0.0)
-        for i in range(BLOCK_HEADS):
-            rows = slice(HEAD * i, HEAD * (i + 1))
-            nc.vector.tensor_copy(out=head_w[rows, :, i], in_=rk_cols[rows, 0 : C // P])
-
         gh = const.tile([P, SEQS, DG], BF16, name="gh")
         nc.scalar.dma_start(out=gh[:], in_=g_hid.rearrange("b n d -> n b d"))
-        gh_ps = ps_one.tile([P, KD, SEQS, P], BF16, name="gh_ps", tag="blocks")
+        gh_ps = ps_work.tile([P, KD, SEQS, P], BF16, name="gh_ps", tag="gate")
         for kd in range(KD):
             for b in range(SEQS):
                 nc.tensor.transpose(gh_ps[:, kd, b, :], gh[:, b, P * kd : P * (kd + 1)], ident_b[:])
         gh_t = const.tile([P, KD, SEQS, P], BF16, name="gh_t")
         nc.vector.tensor_copy(out=gh_t[:], in_=gh_ps[:])
 
+        gam_raw = const.tile([P, PASSES, PACK], BF16, name="gam_raw")
+        bet_raw = const.tile([P, PASSES, PACK], BF16, name="bet_raw")
+        nc.scalar.dma_start(out=gam_raw[:], in_=ln_g.rearrange("(g p t) -> p g t", p=P, t=PACK))
+        nc.scalar.dma_start(out=bet_raw[:], in_=ln_b.rearrange("(g p t) -> p g t", p=P, t=PACK))
+        gam = const.tile([P, PASSES * PACK], F32, name="gam")
+        bet = const.tile([P, PASSES * PACK], F32, name="bet")
+        nc.scalar.copy(out=gam[:], in_=gam_raw[:].rearrange("p g t -> p (g t)"))
+        nc.scalar.copy(out=bet[:], in_=bet_raw[:].rearrange("p g t -> p (g t)"))
+
         w_words = [
             const.tile([P, SLAB_PASSES, CO], U32, name="w_words%d" % s, align_bytes=64)
             for s in range(SLABS)
         ]
-        g2_sorted = [
-            const.tile([P, KD, SLAB_PASSES, PACK, P], BF16, name="g2_sorted%d" % s)
-            for s in range(SLABS)
-        ]
+        g2_cols = [const.tile([P, KD, SLAB], BF16, name="g2_cols%d" % s) for s in range(SLABS)]
+        rk_all = [const.tile([P, SLAB], BF16, name="rk_all%d" % s) for s in range(SLABS)]
 
-        y_of, r_of, k_of, v_of, g2_raw_of = {}, {}, {}, {}, {}
+        y_of, r_of, k_of, v_of, rk_of = {}, {}, {}, {}, {}
         bn_of, var_of, both_of, std_of, rstd_of, shift_of = {}, {}, {}, {}, {}, {}
         words_of, scales_of, acc_of = {}, {}, {}
-        rk_of, rk_ch_of, rk_sb_of, dot_ps_of, dot_of = {}, {}, {}, {}, {}
-        a_tok_of, a_ch_of, yn_of, dv_tok_of, dv_ch_of, y2_of, gate_of = {}, {}, {}, {}, {}, {}, {}
+        dot_of, a_tok_of, a_ch_of, yn_of, dv_tok_of, dv_ch_of, y2_of, gate_of = {}, {}, {}, {}, {}, {}, {}, {}
 
         def slab_cols(u):
             s = u % SLABS
@@ -131,10 +114,14 @@ def tile_full_tmix_params_pc_k_kernel(
             v_of[u] = loads.tile([P, SLAB], BF16, name="v_t")
             nc.sync.dma_start(out=v_of[u][:], in_=v[u // SLABS, :, slab_cols(u)])
 
-        def load_g2(s):
-            g2_raw_of[s] = loads.tile([P, KD, SLAB], BF16, name="g2_raw")
+        def load_r_k(s):
             nc.sync.dma_start(
-                out=g2_raw_of[s][:], in_=g2.rearrange("(kd d) c -> d kd c", kd=KD)[:, :, slab_cols(s)]
+                out=rk_all[s][:], in_=r_k.rearrange("h c -> (h c)")[slab_cols(s)].partition_broadcast(P)
+            )
+
+        def load_g2(s):
+            nc.sync.dma_start(
+                out=g2_cols[s][:], in_=g2.rearrange("(kd d) c -> d kd c", kd=KD)[:, :, slab_cols(s)]
             )
 
         def load_w(s):
@@ -149,50 +136,20 @@ def tile_full_tmix_params_pc_k_kernel(
                 in_=W_o_words[passes].rearrange("g p n t -> p g (n t)").bitcast(I32),
             )
 
-        def sort_g2(j):
-            s, o = j // SLAB_PASSES, j % SLAB_PASSES
-            for kd in range(KD):
-                nc.gpsimd.tensor_scalar(
-                    out=g2_sorted[s][:, kd, o],
-                    in0=g2_raw_of[s][:, kd, PASS * o : PASS * (o + 1)].rearrange(
-                        "d (p t) -> d t p", t=PACK
-                    ),
-                    scalar1=1.0,
-                    scalar2=0.0,
-                    op0=ALU.mult,
-                    op1=ALU.add,
-                )
+        def weighted_products(u):
+            rk_of[u] = loads.tile([P, SLAB], F32, name="rk")
+            nc.gpsimd.tensor_tensor(out=rk_of[u][:], in0=r_of[u][:], in1=k_of[u][:], op=ALU.mult)
+            nc.gpsimd.tensor_tensor(out=rk_of[u][:], in0=rk_of[u][:], in1=rk_all[u % SLABS][:], op=ALU.mult)
 
-        def r_times_k(j):
+        def head_sums(j):
             u, o = j // SLAB_PASSES, j % SLAB_PASSES
-            cols = slice(PASS * o, PASS * (o + 1))
-            rk_of[j] = work.tile([P, PASS], F32, name="rk", bufs=3)
-            nc.gpsimd.tensor_tensor(out=rk_of[j][:], in0=r_of[u][:, cols], in1=k_of[u][:, cols], op=ALU.mult)
-
-        def rk_transpose(j):
-            rk_ch_of[j] = ps_one.tile([P, BANK_BLOCKS, P], F32, name="rk_ch", tag="blocks")
-            for i in range(BANK_BLOCKS):
-                nc.tensor.transpose(rk_ch_of[j][:, i, :], rk_of[j][:, P * i : P * (i + 1)], ident_f[:])
-
-        def rk_copy(j):
-            rk_sb_of[j] = work.tile([P, BANK_BLOCKS, P], F32, name="rk_sb", bufs=3)
-            nc.scalar.copy(out=rk_sb_of[j][:], in_=rk_ch_of[j][:])
-
-        def dot_matmul(j):
-            g = j % PASSES
-            dot_ps_of[j] = ps_one.tile([P, PASS_HEADS], F32, name="dot_ps")
-            for i in range(BANK_BLOCKS):
-                nc.tensor.matmul(
-                    out=dot_ps_of[j][:, BLOCK_HEADS * i : BLOCK_HEADS * (i + 1)],
-                    lhsT=rk_sb_of[j][:, i, :],
-                    rhs=head_w[:, BANK_BLOCKS * g + i, :],
-                    start=True,
-                    stop=True,
-                )
-
-        def dot_copy(j):
             dot_of[j] = stats.tile([P, PASS_HEADS], F32, name="dot", bufs=3)
-            nc.vector.tensor_copy(out=dot_of[j][:], in_=dot_ps_of[j][:])
+            nc.vector.tensor_reduce(
+                out=dot_of[j][:],
+                in_=rk_of[u][:, PASS * o : PASS * (o + 1)].rearrange("n (h c) -> n h c", c=HEAD),
+                axis=AX.X,
+                op=ALU.add,
+            )
 
         def y_stats(j):
             u = j // SLAB_PASSES
@@ -251,7 +208,7 @@ def tile_full_tmix_params_pc_k_kernel(
                 )
 
         def a_transpose(j):
-            a_ch_of[j] = ps_a.tile([P, PACK, P], F32, name="a_ch")
+            a_ch_of[j] = ps_work.tile([P, PACK, P], F32, name="a_ch")
             for t in range(PACK):
                 nc.tensor.transpose(a_ch_of[j][:, t, :], a_tok_of[j][:, t, :], ident_f[:])
 
@@ -280,19 +237,19 @@ def tile_full_tmix_params_pc_k_kernel(
                 )
 
         def dv_transpose(j):
-            dv_ch_of[j] = ps_one.tile([P, PACK, P], F32, name="dv_ch")
+            dv_ch_of[j] = ps_work.tile([P, PACK, P], F32, name="dv_ch")
             for t in range(PACK):
                 nc.tensor.transpose(dv_ch_of[j][:, t, :], dv_tok_of[j][:, t, :], ident_f[:])
 
         def gate_matmul(j):
             b, g = j // PASSES, j % PASSES
             s, o = g // SLAB_PASSES, g % SLAB_PASSES
-            gate_of[j] = ps_one.tile([P, PACK, P], F32, name="gate")
+            gate_of[j] = ps_work.tile([P, PACK, P], F32, name="gate")
             for t in range(PACK):
                 for kd in range(KD):
                     nc.tensor.matmul(
                         out=gate_of[j][:, t, :],
-                        lhsT=g2_sorted[s][:, kd, o, t, :],
+                        lhsT=g2_cols[s][:, kd, PASS * o + t : PASS * (o + 1) : PACK],
                         rhs=gh_t[:, kd, b, :],
                         start=(kd == 0),
                         stop=(kd == KD - 1),
@@ -352,58 +309,49 @@ def tile_full_tmix_params_pc_k_kernel(
             first = tick + lead
             return [first // SLAB_PASSES] if first % SLAB_PASSES == 0 and 0 <= first < SLAB_PASSES * slabs else []
 
-        for tick in range(-12, STEPS + 5):
-            for u in slab_due(tick, 12, SEQS * SLABS):
+        for tick in range(-11, STEPS + 3):
+            for u in slab_due(tick, 11, SEQS * SLABS):
                 load_y_r_k(u)
-            for s in slab_due(tick, 8, SLABS):
+            for s in slab_due(tick, 11, SLABS):
+                load_r_k(s)
+            for s in slab_due(tick, 5, SLABS):
                 load_g2(s)
-            for u in slab_due(tick, 7, SEQS * SLABS):
+            for u in slab_due(tick, 6, SEQS * SLABS):
                 load_v(u)
             for s in slab_due(tick, 2, SLABS):
                 load_w(s)
 
             for j in step_due(tick, 0):
                 add_bonus(j)
-            for j in step_due(tick, 3):
-                dot_copy(j)
-            for u in slab_due(tick, 4, SEQS * SLABS):
-                scale_and_shift(u)
-            for j in step_due(tick, 8):
-                y_stats(j)
-            for u in slab_due(tick, 5, SEQS * SLABS):
-                variance(u)
-            for j in step_due(tick, 0):
                 gated_and_quantised(j)
+            for j in step_due(tick, 3):
+                head_sums(j)
+            for u in slab_due(tick, 3, SEQS * SLABS):
+                scale_and_shift(u)
+            for j in step_due(tick, 7):
+                y_stats(j)
+            for u in slab_due(tick, 4, SEQS * SLABS):
+                variance(u)
 
             for j in step_due(tick, 1):
                 gain_and_bias(j)
             for b in range(SEQS):
-                if tick == PASSES * (b + 1) + 4:
+                if tick == PASSES * (b + 1) + 2:
                     store(b)
-            for j in step_due(tick, 5):
-                rk_copy(j)
-            for u in slab_due(tick, 5, SEQS * SLABS):
-                root(u)
-            for j in step_due(tick, 3):
+            for j in step_due(tick, 2):
                 dot_times_v(j)
-            for j in step_due(tick, 4):
+            for j in step_due(tick, 3):
                 normalise(j)
+            for u in slab_due(tick, 4, SEQS * SLABS):
+                root(u)
 
+            for u in slab_due(tick, -SLAB_PASSES, SEQS * SLABS):
+                project(u)
             for j in step_due(tick, 1):
                 dv_transpose(j)
-            for j in step_due(tick, 4):
-                dot_matmul(j)
+                gate_matmul(j)
             for j in step_due(tick, 2):
                 a_transpose(j)
-            for j in step_due(tick, 1):
-                gate_matmul(j)
-            for j in step_due(tick, 6):
-                rk_transpose(j)
-            for u in slab_due(tick, -6, SEQS * SLABS):
-                project(u)
 
-            for j in step_due(tick, 8):
-                r_times_k(j)
-            for j in step_due(tick, 4):
-                if j < PASSES:
-                    sort_g2(j)
+            for u in slab_due(tick, 8, SEQS * SLABS):
+                weighted_products(u)

@@ -49,7 +49,8 @@ def tile_full_tmix_params_pc_k_kernel(
         stats = ctx.enter_context(tc.tile_pool(name="stats", bufs=2))
         work = ctx.enter_context(tc.tile_pool(name="work", bufs=2))
         ps_acc = ctx.enter_context(tc.psum_pool(name="ps_acc", bufs=1))
-        ps_work = ctx.enter_context(tc.psum_pool(name="ps_work", bufs=2))
+        ps_a = ctx.enter_context(tc.psum_pool(name="ps_a", bufs=2))
+        ps_one = ctx.enter_context(tc.psum_pool(name="ps_one", bufs=1))
         ctx.enter_context(tc.manual_schedule())
 
         ident_f = const.tile([P, P], F32, name="ident_f")
@@ -60,9 +61,22 @@ def tile_full_tmix_params_pc_k_kernel(
         planes = const.tile([P, SLABS, CO], U8, name="planes", align_bytes=64)
         nc.vector.memset(planes[:].bitcast(I32), 0)
 
+        rk_rows = const.tile([P, P], BF16, name="rk_rows")
+        nc.vector.memset(rk_rows[:], 0.0)
+        nc.scalar.dma_start(
+            out=rk_rows[0 : C // P, :], in_=r_k.rearrange("(j i) c -> j (i c)", i=BLOCK_HEADS)
+        )
         gh = const.tile([P, SEQS, DG], BF16, name="gh")
         nc.scalar.dma_start(out=gh[:], in_=g_hid.rearrange("b n d -> n b d"))
-        gh_ps = ps_work.tile([P, KD, SEQS, P], BF16, name="gh_ps", tag="gate")
+        rk_cols = ps_one.tile([P, P], BF16, name="rk_cols", tag="blocks")
+        nc.tensor.transpose(rk_cols[:], rk_rows[:], ident_b[:])
+        head_w = const.tile([P, C // P, BLOCK_HEADS], F32, name="head_w")
+        nc.vector.memset(head_w[:], 0.0)
+        for i in range(BLOCK_HEADS):
+            rows = slice(HEAD * i, HEAD * (i + 1))
+            nc.vector.tensor_copy(out=head_w[rows, :, i], in_=rk_cols[rows, 0 : C // P])
+
+        gh_ps = ps_one.tile([P, KD, SEQS, P], BF16, name="gh_ps", tag="blocks")
         for kd in range(KD):
             for b in range(SEQS):
                 nc.tensor.transpose(gh_ps[:, kd, b, :], gh[:, b, P * kd : P * (kd + 1)], ident_b[:])
@@ -82,13 +96,16 @@ def tile_full_tmix_params_pc_k_kernel(
             const.tile([P, SLAB_PASSES, CO], U32, name="w_words%d" % s, align_bytes=64)
             for s in range(SLABS)
         ]
-        g2_cols = [const.tile([P, KD, SLAB], BF16, name="g2_cols%d" % s) for s in range(SLABS)]
-        rk_all = [const.tile([P, SLAB], BF16, name="rk_all%d" % s) for s in range(SLABS)]
+        g2_sorted = [
+            const.tile([P, KD, SLAB_PASSES, PACK, P], BF16, name="g2_sorted%d" % s)
+            for s in range(SLABS)
+        ]
 
-        y_of, r_of, k_of, v_of, rk_of = {}, {}, {}, {}, {}
+        y_of, r_of, k_of, v_of, g2_raw_of = {}, {}, {}, {}, {}
         bn_of, var_of, both_of, std_of, rstd_of, shift_of = {}, {}, {}, {}, {}, {}
         words_of, scales_of, acc_of = {}, {}, {}
-        dot_of, a_tok_of, a_ch_of, yn_of, dv_tok_of, dv_ch_of, y2_of, gate_of = {}, {}, {}, {}, {}, {}, {}, {}
+        rk_of, rk_ch_of, rk_sb_of, dot_ps_of, dot_of = {}, {}, {}, {}, {}
+        a_tok_of, a_ch_of, yn_of, dv_tok_of, dv_ch_of, y2_of, gate_of = {}, {}, {}, {}, {}, {}, {}
 
         def slab_cols(u):
             s = u % SLABS
@@ -114,14 +131,10 @@ def tile_full_tmix_params_pc_k_kernel(
             v_of[u] = loads.tile([P, SLAB], BF16, name="v_t")
             nc.sync.dma_start(out=v_of[u][:], in_=v[u // SLABS, :, slab_cols(u)])
 
-        def load_r_k(s):
-            nc.sync.dma_start(
-                out=rk_all[s][:], in_=r_k.rearrange("h c -> (h c)")[slab_cols(s)].partition_broadcast(P)
-            )
-
         def load_g2(s):
+            g2_raw_of[s] = loads.tile([P, KD, SLAB], BF16, name="g2_raw")
             nc.sync.dma_start(
-                out=g2_cols[s][:], in_=g2.rearrange("(kd d) c -> d kd c", kd=KD)[:, :, slab_cols(s)]
+                out=g2_raw_of[s][:], in_=g2.rearrange("(kd d) c -> d kd c", kd=KD)[:, :, slab_cols(s)]
             )
 
         def load_w(s):
@@ -136,20 +149,50 @@ def tile_full_tmix_params_pc_k_kernel(
                 in_=W_o_words[passes].rearrange("g p n t -> p g (n t)").bitcast(I32),
             )
 
-        def weighted_products(u):
-            rk_of[u] = loads.tile([P, SLAB], F32, name="rk")
-            nc.gpsimd.tensor_tensor(out=rk_of[u][:], in0=r_of[u][:], in1=k_of[u][:], op=ALU.mult)
-            nc.gpsimd.tensor_tensor(out=rk_of[u][:], in0=rk_of[u][:], in1=rk_all[u % SLABS][:], op=ALU.mult)
+        def sort_g2(j):
+            s, o = j // SLAB_PASSES, j % SLAB_PASSES
+            for kd in range(KD):
+                nc.gpsimd.tensor_scalar(
+                    out=g2_sorted[s][:, kd, o],
+                    in0=g2_raw_of[s][:, kd, PASS * o : PASS * (o + 1)].rearrange(
+                        "d (p t) -> d t p", t=PACK
+                    ),
+                    scalar1=1.0,
+                    scalar2=0.0,
+                    op0=ALU.mult,
+                    op1=ALU.add,
+                )
 
-        def head_sums(j):
+        def r_times_k(j):
             u, o = j // SLAB_PASSES, j % SLAB_PASSES
+            cols = slice(PASS * o, PASS * (o + 1))
+            rk_of[j] = work.tile([P, PASS], F32, name="rk", bufs=3)
+            nc.gpsimd.tensor_tensor(out=rk_of[j][:], in0=r_of[u][:, cols], in1=k_of[u][:, cols], op=ALU.mult)
+
+        def rk_transpose(j):
+            rk_ch_of[j] = ps_one.tile([P, BANK_BLOCKS, P], F32, name="rk_ch", tag="blocks")
+            for i in range(BANK_BLOCKS):
+                nc.tensor.transpose(rk_ch_of[j][:, i, :], rk_of[j][:, P * i : P * (i + 1)], ident_f[:])
+
+        def rk_copy(j):
+            rk_sb_of[j] = work.tile([P, BANK_BLOCKS, P], F32, name="rk_sb", bufs=3)
+            nc.scalar.copy(out=rk_sb_of[j][:], in_=rk_ch_of[j][:])
+
+        def dot_matmul(j):
+            g = j % PASSES
+            dot_ps_of[j] = ps_one.tile([P, PASS_HEADS], F32, name="dot_ps")
+            for i in range(BANK_BLOCKS):
+                nc.tensor.matmul(
+                    out=dot_ps_of[j][:, BLOCK_HEADS * i : BLOCK_HEADS * (i + 1)],
+                    lhsT=rk_sb_of[j][:, i, :],
+                    rhs=head_w[:, BANK_BLOCKS * g + i, :],
+                    start=True,
+                    stop=True,
+                )
+
+        def dot_copy(j):
             dot_of[j] = stats.tile([P, PASS_HEADS], F32, name="dot", bufs=3)
-            nc.vector.tensor_reduce(
-                out=dot_of[j][:],
-                in_=rk_of[u][:, PASS * o : PASS * (o + 1)].rearrange("n (h c) -> n h c", c=HEAD),
-                axis=AX.X,
-                op=ALU.add,
-            )
+            nc.vector.tensor_copy(out=dot_of[j][:], in_=dot_ps_of[j][:])
 
         def y_stats(j):
             u = j // SLAB_PASSES
@@ -208,7 +251,7 @@ def tile_full_tmix_params_pc_k_kernel(
                 )
 
         def a_transpose(j):
-            a_ch_of[j] = ps_work.tile([P, PACK, P], F32, name="a_ch")
+            a_ch_of[j] = ps_a.tile([P, PACK, P], F32, name="a_ch")
             for t in range(PACK):
                 nc.tensor.transpose(a_ch_of[j][:, t, :], a_tok_of[j][:, t, :], ident_f[:])
 
@@ -237,19 +280,19 @@ def tile_full_tmix_params_pc_k_kernel(
                 )
 
         def dv_transpose(j):
-            dv_ch_of[j] = ps_work.tile([P, PACK, P], F32, name="dv_ch")
+            dv_ch_of[j] = ps_one.tile([P, PACK, P], F32, name="dv_ch")
             for t in range(PACK):
                 nc.tensor.transpose(dv_ch_of[j][:, t, :], dv_tok_of[j][:, t, :], ident_f[:])
 
         def gate_matmul(j):
             b, g = j // PASSES, j % PASSES
             s, o = g // SLAB_PASSES, g % SLAB_PASSES
-            gate_of[j] = ps_work.tile([P, PACK, P], F32, name="gate")
+            gate_of[j] = ps_one.tile([P, PACK, P], F32, name="gate")
             for t in range(PACK):
                 for kd in range(KD):
                     nc.tensor.matmul(
                         out=gate_of[j][:, t, :],
-                        lhsT=g2_cols[s][:, kd, PASS * o + t : PASS * (o + 1) : PACK],
+                        lhsT=g2_sorted[s][:, kd, o, t, :],
                         rhs=gh_t[:, kd, b, :],
                         start=(kd == 0),
                         stop=(kd == KD - 1),
@@ -281,10 +324,10 @@ def tile_full_tmix_params_pc_k_kernel(
             b, s = u // SLABS, u % SLABS
             if s == 0:
                 acc_of[b] = [ps_acc.tile([P, N_TILE], F32, name="acc%d" % half) for half in range(HALVES)]
-            for o in range(SLAB_PASSES):
-                g = SLAB_PASSES * s + o
-                for half in range(HALVES):
-                    n_cols = slice(N_TILE * half, N_TILE * (half + 1))
+            for half in range(HALVES):
+                n_cols = slice(N_TILE * half, N_TILE * (half + 1))
+                for o in range(SLAB_PASSES):
+                    g = SLAB_PASSES * s + o
                     nc.tensor.matmul_mx(
                         out=acc_of[b][half][:],
                         lhsT=words_of[u][:, o, :].bitcast(FP8X4),
@@ -309,49 +352,58 @@ def tile_full_tmix_params_pc_k_kernel(
             first = tick + lead
             return [first // SLAB_PASSES] if first % SLAB_PASSES == 0 and 0 <= first < SLAB_PASSES * slabs else []
 
-        for tick in range(-11, STEPS + 3):
-            for u in slab_due(tick, 11, SEQS * SLABS):
+        for tick in range(-12, STEPS + 5):
+            for u in slab_due(tick, 12, SEQS * SLABS):
                 load_y_r_k(u)
-            for s in slab_due(tick, 11, SLABS):
-                load_r_k(s)
-            for s in slab_due(tick, 5, SLABS):
+            for s in slab_due(tick, 8, SLABS):
                 load_g2(s)
-            for u in slab_due(tick, 6, SEQS * SLABS):
+            for u in slab_due(tick, 7, SEQS * SLABS):
                 load_v(u)
             for s in slab_due(tick, 2, SLABS):
                 load_w(s)
 
             for j in step_due(tick, 0):
                 add_bonus(j)
-                gated_and_quantised(j)
             for j in step_due(tick, 3):
-                head_sums(j)
-            for u in slab_due(tick, 3, SEQS * SLABS):
-                scale_and_shift(u)
-            for j in step_due(tick, 7):
-                y_stats(j)
+                dot_copy(j)
             for u in slab_due(tick, 4, SEQS * SLABS):
+                scale_and_shift(u)
+            for j in step_due(tick, 8):
+                y_stats(j)
+            for u in slab_due(tick, 5, SEQS * SLABS):
                 variance(u)
+            for j in step_due(tick, 0):
+                gated_and_quantised(j)
 
             for j in step_due(tick, 1):
                 gain_and_bias(j)
             for b in range(SEQS):
-                if tick == PASSES * (b + 1) + 2:
+                if tick == PASSES * (b + 1) + 4:
                     store(b)
-            for j in step_due(tick, 2):
-                dot_times_v(j)
-            for j in step_due(tick, 3):
-                normalise(j)
-            for u in slab_due(tick, 4, SEQS * SLABS):
+            for j in step_due(tick, 5):
+                rk_copy(j)
+            for u in slab_due(tick, 5, SEQS * SLABS):
                 root(u)
+            for j in step_due(tick, 3):
+                dot_times_v(j)
+            for j in step_due(tick, 4):
+                normalise(j)
 
-            for u in slab_due(tick, -SLAB_PASSES, SEQS * SLABS):
-                project(u)
             for j in step_due(tick, 1):
                 dv_transpose(j)
-                gate_matmul(j)
+            for j in step_due(tick, 4):
+                dot_matmul(j)
             for j in step_due(tick, 2):
                 a_transpose(j)
+            for j in step_due(tick, 1):
+                gate_matmul(j)
+            for j in step_due(tick, 6):
+                rk_transpose(j)
+            for u in slab_due(tick, -6, SEQS * SLABS):
+                project(u)
 
-            for u in slab_due(tick, 8, SEQS * SLABS):
-                weighted_products(u)
+            for j in step_due(tick, 8):
+                r_times_k(j)
+            for j in step_due(tick, 4):
+                if j < PASSES:
+                    sort_g2(j)

@@ -96,13 +96,10 @@ def tile_full_tmix_params_pc_k_kernel(
             const.tile([P, SLAB_PASSES, CO], U32, name="w_words%d" % s, align_bytes=64)
             for s in range(SLABS)
         ]
-        g2_sorted = [
-            const.tile([P, KD, SLAB_PASSES, PACK, P], BF16, name="g2_sorted%d" % s)
-            for s in range(SLABS)
-        ]
+        g2_rows = [const.tile([P, KD, SLAB], BF16, name="g2_rows%d" % s) for s in range(SLABS)]
 
-        y_of, r_of, k_of, v_of, g2_raw_of = {}, {}, {}, {}, {}
-        bn_of, var_of, both_of, std_of, rstd_of, shift_of = {}, {}, {}, {}, {}, {}
+        y_of, r_of, k_of, v_of = {}, {}, {}, {}
+        bn_of, var_of, std_of, rstd_of, shift_of = {}, {}, {}, {}, {}
         words_of, scales_of, acc_of = {}, {}, {}
         rk_of, rk_ch_of, rk_sb_of, dot_ps_of, dot_of = {}, {}, {}, {}, {}
         a_tok_of, a_ch_of, yn_of, dv_tok_of, dv_ch_of, y2_of, gate_of = {}, {}, {}, {}, {}, {}, {}
@@ -132,9 +129,8 @@ def tile_full_tmix_params_pc_k_kernel(
             nc.sync.dma_start(out=v_of[u][:], in_=v[u // SLABS, :, slab_cols(u)])
 
         def load_g2(s):
-            g2_raw_of[s] = loads.tile([P, KD, SLAB], BF16, name="g2_raw")
             nc.sync.dma_start(
-                out=g2_raw_of[s][:], in_=g2.rearrange("(kd d) c -> d kd c", kd=KD)[:, :, slab_cols(s)]
+                out=g2_rows[s][:], in_=g2.rearrange("(kd d) c -> d kd c", kd=KD)[:, :, slab_cols(s)]
             )
 
         def load_w(s):
@@ -148,20 +144,6 @@ def tile_full_tmix_params_pc_k_kernel(
                 out=w_words[s][:].bitcast(I32),
                 in_=W_o_words[passes].rearrange("g p n t -> p g (n t)").bitcast(I32),
             )
-
-        def sort_g2(j):
-            s, o = j // SLAB_PASSES, j % SLAB_PASSES
-            for kd in range(KD):
-                nc.gpsimd.tensor_scalar(
-                    out=g2_sorted[s][:, kd, o],
-                    in0=g2_raw_of[s][:, kd, PASS * o : PASS * (o + 1)].rearrange(
-                        "d (p t) -> d t p", t=PACK
-                    ),
-                    scalar1=1.0,
-                    scalar2=0.0,
-                    op0=ALU.mult,
-                    op1=ALU.add,
-                )
 
         def r_times_k(j):
             u, o = j // SLAB_PASSES, j % SLAB_PASSES
@@ -197,29 +179,23 @@ def tile_full_tmix_params_pc_k_kernel(
         def y_stats(j):
             u = j // SLAB_PASSES
             if j % SLAB_PASSES == 0:
-                bn_of[u] = stats.tile([P, SLAB_HEADS, 6], F32, name="bn")
-            for h in step_heads(j):
-                nc.vector.bn_stats(out=bn_of[u][:, h, :], in_=y_of[u][:, HEAD * h : HEAD * (h + 1)])
+                bn_of[u] = stats.tile([P, SLAB_HEADS, 3], F32, name="bn")
+            for h in step_heads(j)[::2]:
+                nc.vector.bn_stats(
+                    out=bn_of[u][:, h : h + 2, :].rearrange("n h s -> n (h s)"),
+                    in_=y_of[u][:, HEAD * h : HEAD * (h + 2)].rearrange("n (h c) -> n c h", h=2),
+                )
 
         def variance(u):
-            bn = bn_of[u]
-            both = stats.tile([P, SLAB_HEADS, 3], F32, name="both")
-            nc.vector.tensor_reduce(
-                out=both[:], in_=bn[:].rearrange("n h (e s) -> n h s e", e=2), axis=AX.X, op=ALU.add
-            )
-            gap = stats.tile([P, SLAB_HEADS], F32, name="gap")
-            nc.vector.tensor_tensor(out=gap[:], in0=bn[:, :, 1], in1=bn[:, :, 4], op=ALU.subtract)
-            gap2 = stats.tile([P, SLAB_HEADS], F32, name="gap2")
-            nc.vector.scalar_tensor_tensor(
-                out=gap2[:], in0=gap[:], scalar=0.25, in1=gap[:], op0=ALU.mult, op1=ALU.mult
-            )
-            within = stats.tile([P, SLAB_HEADS], F32, name="within")
-            nc.vector.tensor_scalar(
-                out=within[:], in0=both[:, :, 2], scalar1=1.0 / HEAD, scalar2=EPS, op0=ALU.mult, op1=ALU.add
-            )
             var_of[u] = stats.tile([P, SLAB_HEADS], F32, name="var_eps")
-            nc.vector.tensor_tensor(out=var_of[u][:], in0=gap2[:], in1=within[:], op=ALU.add)
-            both_of[u] = both
+            nc.vector.tensor_scalar(
+                out=var_of[u][:],
+                in0=bn_of[u][:, :, 2],
+                scalar1=1.0 / HEAD,
+                scalar2=EPS,
+                op0=ALU.mult,
+                op1=ALU.add,
+            )
 
         def root(u):
             std_of[u] = stats.tile([P, SLAB_HEADS], F32, name="std")
@@ -231,8 +207,8 @@ def tile_full_tmix_params_pc_k_kernel(
             shift_of[u] = stats.tile([P, SLAB_HEADS], F32, name="shift")
             nc.vector.scalar_tensor_tensor(
                 out=shift_of[u][:],
-                in0=both_of[u][:, :, 1],
-                scalar=-0.5,
+                in0=bn_of[u][:, :, 1],
+                scalar=-1.0,
                 in1=rstd_of[u][:],
                 op0=ALU.mult,
                 op1=ALU.mult,
@@ -271,13 +247,15 @@ def tile_full_tmix_params_pc_k_kernel(
         def dot_times_v(j):
             u = j // SLAB_PASSES
             dv_tok_of[j] = work.tile([P, PACK, P], F32, name="dv_tok", bufs=3)
-            for hh, h in enumerate(step_heads(j)):
-                nc.scalar.activation(
-                    out=dv_tok_of[j][:, :, HEAD_PARTS * hh : HEAD_PARTS * (hh + 1)],
-                    in_=by_value(v_of[u][:, HEAD * h : HEAD * (h + 1)]),
-                    func=ACT.Copy,
-                    scale=dot_of[j][:, hh : hh + 1],
-                )
+            o = j % SLAB_PASSES
+            nc.gpsimd.tensor_tensor(
+                out=dv_tok_of[j][:].rearrange("n t (h p) -> n t h p", p=HEAD_PARTS),
+                in0=v_of[u][:, PASS * o : PASS * (o + 1)].rearrange(
+                    "n (h p t) -> n t h p", p=HEAD_PARTS, t=PACK
+                ),
+                in1=dot_of[j][:].unsqueeze(1).unsqueeze(3).to_broadcast([P, PACK, PASS_HEADS, HEAD_PARTS]),
+                op=ALU.mult,
+            )
 
         def dv_transpose(j):
             dv_ch_of[j] = ps_one.tile([P, PACK, P], F32, name="dv_ch")
@@ -292,7 +270,7 @@ def tile_full_tmix_params_pc_k_kernel(
                 for kd in range(KD):
                     nc.tensor.matmul(
                         out=gate_of[j][:, t, :],
-                        lhsT=g2_sorted[s][:, kd, o, t, :],
+                        lhsT=g2_rows[s][:, kd, PASS * o + t : PASS * (o + 1) : PACK],
                         rhs=gh_t[:, kd, b, :],
                         start=(kd == 0),
                         stop=(kd == KD - 1),
@@ -384,8 +362,6 @@ def tile_full_tmix_params_pc_k_kernel(
                 rk_copy(j)
             for u in slab_due(tick, 5, SEQS * SLABS):
                 root(u)
-            for j in step_due(tick, 3):
-                dot_times_v(j)
             for j in step_due(tick, 4):
                 normalise(j)
 
@@ -404,6 +380,5 @@ def tile_full_tmix_params_pc_k_kernel(
 
             for j in step_due(tick, 8):
                 r_times_k(j)
-            for j in step_due(tick, 4):
-                if j < PASSES:
-                    sort_g2(j)
+            for j in step_due(tick, 3):
+                dot_times_v(j)

@@ -120,9 +120,14 @@ def tile_full_tmix_params_pc_k_kernel(
             y_of[u] = loads.tile([P, SLAB], BF16, name="y_t", bufs=3)
             r_of[u] = loads.tile([P, SLAB], BF16, name="r_t")
             k_of[u] = loads.tile([P, SLAB], BF16, name="k_t")
-            nc.sync.dma_start(out=y_of[u][:], in_=y[b, :, slab_cols(u)])
-            nc.sync.dma_start(out=r_of[u][:], in_=r[b, :, slab_cols(u)])
-            nc.sync.dma_start(out=k_of[u][:], in_=k[b, :, slab_cols(u)])
+            pieces = SLAB_PASSES if u == 0 else 1
+            width = SLAB // pieces
+            for piece in range(pieces):
+                in_tile = slice(width * piece, width * (piece + 1))
+                in_hbm = slice(SLAB * (u % SLABS) + width * piece, SLAB * (u % SLABS) + width * (piece + 1))
+                nc.sync.dma_start(out=r_of[u][:, in_tile], in_=r[b, :, in_hbm])
+                nc.sync.dma_start(out=k_of[u][:, in_tile], in_=k[b, :, in_hbm])
+                nc.sync.dma_start(out=y_of[u][:, in_tile], in_=y[b, :, in_hbm])
 
         def load_v(u):
             v_of[u] = loads.tile([P, SLAB], BF16, name="v_t")
@@ -281,10 +286,8 @@ def tile_full_tmix_params_pc_k_kernel(
             nc.vector.tensor_tensor(out=y2_of[j][:], in0=yn_of[j][:], in1=dv_ch_of[j][:], op=ALU.add)
 
         def gated_and_quantised(j):
-            u, o = j // SLAB_PASSES, j % SLAB_PASSES
-            if o == 0:
-                words_of[u] = work.tile([P, SLAB_PASSES, P], U32, name="z_words", align_bytes=64)
-                scales_of[u] = work.tile([P, SLAB_PASSES, P], U8, name="z_scales", align_bytes=64)
+            words_of[j] = work.tile([P, P], U32, name="z_words", align_bytes=64, bufs=7)
+            scales_of[j] = work.tile([P, P], U8, name="z_scales", align_bytes=64, bufs=7)
             z_bf = work.tile([P, P, PACK], BF16, name="z_bf", align_bytes=64)
             nc.vector.tensor_tensor(
                 out=z_bf[:],
@@ -293,28 +296,30 @@ def tile_full_tmix_params_pc_k_kernel(
                 op=ALU.mult,
             )
             nc.vector.quantize_mx(
-                out=words_of[u][:, o, :].bitcast(FP8X4),
-                scales=scales_of[u][:, o, :],
+                out=words_of[j][:].bitcast(FP8X4),
+                scales=scales_of[j][:],
                 in_=z_bf[:].rearrange("p n t -> p (n t)"),
             )
 
-        def project(u):
-            b, s = u // SLABS, u % SLABS
-            if s == 0:
+        def project(j):
+            b, g = j // PASSES, j % PASSES
+            s, o = g // SLAB_PASSES, g % SLAB_PASSES
+            if g == 0:
                 acc_of[b] = [ps_acc.tile([P, N_TILE], F32, name="acc%d" % half) for half in range(HALVES)]
             for half in range(HALVES):
                 n_cols = slice(N_TILE * half, N_TILE * (half + 1))
-                for o in range(SLAB_PASSES):
-                    g = SLAB_PASSES * s + o
-                    nc.tensor.matmul_mx(
-                        out=acc_of[b][half][:],
-                        lhsT=words_of[u][:, o, :].bitcast(FP8X4),
-                        lhsT_scale=scales_of[u][:, o, :],
-                        rhs=w_words[s][:, o, n_cols].bitcast(FP8X4),
-                        rhs_scale=planes[4 * o : P, s, n_cols],
-                        start=(g == 0),
-                        stop=(g == PASSES - 1),
-                    )
+                nc.tensor.matmul_mx(
+                    out=acc_of[b][half][:],
+                    lhsT=words_of[j][:].bitcast(FP8X4),
+                    lhsT_scale=scales_of[j][:],
+                    rhs=w_words[s][:, o, n_cols].bitcast(FP8X4),
+                    rhs_scale=planes[4 * o : P, s, n_cols],
+                    start=(g == 0),
+                    stop=(g == PASSES - 1),
+                )
+
+        def projection_lag(j):
+            return 4 - max(0, j // SLAB_PASSES - SLABS)
 
         def store(b):
             for half in range(HALVES):
@@ -337,7 +342,7 @@ def tile_full_tmix_params_pc_k_kernel(
                 load_g2(s)
             for u in slab_due(tick, 7, SEQS * SLABS):
                 load_v(u)
-            for s in slab_due(tick, 2, SLABS):
+            for s in slab_due(tick, 4, SLABS):
                 load_w(s)
 
             for j in step_due(tick, 0):
@@ -365,18 +370,19 @@ def tile_full_tmix_params_pc_k_kernel(
             for j in step_due(tick, 4):
                 normalise(j)
 
+            for j in step_due(tick, 2):
+                a_transpose(j)
             for j in step_due(tick, 1):
                 dv_transpose(j)
             for j in step_due(tick, 4):
                 dot_matmul(j)
-            for j in step_due(tick, 2):
-                a_transpose(j)
+            for j in range(STEPS):
+                if j + projection_lag(j) == tick:
+                    project(j)
             for j in step_due(tick, 1):
                 gate_matmul(j)
             for j in step_due(tick, 6):
                 rk_transpose(j)
-            for u in slab_due(tick, -6, SEQS * SLABS):
-                project(u)
 
             for j in step_due(tick, 8):
                 r_times_k(j)

@@ -49,7 +49,7 @@ def tile_full_tmix_params_pc_k_kernel(
         stats = ctx.enter_context(tc.tile_pool(name="stats", bufs=2))
         work = ctx.enter_context(tc.tile_pool(name="work", bufs=2))
         ps_acc = ctx.enter_context(tc.psum_pool(name="ps_acc", bufs=1))
-        ps_a = ctx.enter_context(tc.psum_pool(name="ps_a", bufs=2))
+        ps_rk = ctx.enter_context(tc.psum_pool(name="ps_rk", bufs=2))
         ps_one = ctx.enter_context(tc.psum_pool(name="ps_one", bufs=1))
         ctx.enter_context(tc.manual_schedule())
 
@@ -68,15 +68,15 @@ def tile_full_tmix_params_pc_k_kernel(
         )
         gh = const.tile([P, SEQS, DG], BF16, name="gh")
         nc.scalar.dma_start(out=gh[:], in_=g_hid.rearrange("b n d -> n b d"))
-        rk_cols = ps_one.tile([P, P], BF16, name="rk_cols", tag="blocks")
+        rk_cols = ps_rk.tile([P, P], BF16, name="rk_cols", tag="rk_ch")
         nc.tensor.transpose(rk_cols[:], rk_rows[:], ident_b[:])
-        head_w = const.tile([P, C // P, BLOCK_HEADS], F32, name="head_w")
+        head_w = const.tile([P, C // P, BLOCK_HEADS], BF16, name="head_w")
         nc.vector.memset(head_w[:], 0.0)
         for i in range(BLOCK_HEADS):
             rows = slice(HEAD * i, HEAD * (i + 1))
             nc.vector.tensor_copy(out=head_w[rows, :, i], in_=rk_cols[rows, 0 : C // P])
 
-        gh_ps = ps_one.tile([P, KD, SEQS, P], BF16, name="gh_ps", tag="blocks")
+        gh_ps = ps_rk.tile([P, KD, SEQS, P], BF16, name="gh_ps", tag="rk_ch")
         for kd in range(KD):
             for b in range(SEQS):
                 nc.tensor.transpose(gh_ps[:, kd, b, :], gh[:, b, P * kd : P * (kd + 1)], ident_b[:])
@@ -100,8 +100,8 @@ def tile_full_tmix_params_pc_k_kernel(
 
         y_of, r_of, k_of, v_of = {}, {}, {}, {}
         bn_of, var_of, std_of, rstd_of, shift_of = {}, {}, {}, {}, {}
-        words_of, scales_of, acc_of = {}, {}, {}
-        rk_of, rk_ch_of, rk_sb_of, dot_ps_of, dot_of = {}, {}, {}, {}, {}
+        z_of, words_of, scales_of, acc_of = {}, {}, {}, {}
+        rk_of, rk_ch_of, high_of, low_of, dot_ps_of, dot_of = {}, {}, {}, {}, {}, {}
         a_tok_of, a_ch_of, yn_of, dv_tok_of, dv_ch_of, y2_of, gate_of = {}, {}, {}, {}, {}, {}, {}
 
         def slab_cols(u):
@@ -117,9 +117,9 @@ def tile_full_tmix_params_pc_k_kernel(
 
         def load_y_r_k(u):
             b = u // SLABS
-            y_of[u] = loads.tile([P, SLAB], BF16, name="y_t", bufs=3)
-            r_of[u] = loads.tile([P, SLAB], BF16, name="r_t")
-            k_of[u] = loads.tile([P, SLAB], BF16, name="k_t")
+            y_of[u] = loads.tile([P, SLAB], BF16, name="y_t", bufs=4)
+            r_of[u] = loads.tile([P, SLAB], BF16, name="r_t", bufs=4)
+            k_of[u] = loads.tile([P, SLAB], BF16, name="k_t", bufs=4)
             pieces = SLAB_PASSES if u == 0 else 1
             width = SLAB // pieces
             for piece in range(pieces):
@@ -130,7 +130,7 @@ def tile_full_tmix_params_pc_k_kernel(
                 nc.sync.dma_start(out=y_of[u][:, in_tile], in_=y[b, :, in_hbm])
 
         def load_v(u):
-            v_of[u] = loads.tile([P, SLAB], BF16, name="v_t")
+            v_of[u] = loads.tile([P, SLAB], BF16, name="v_t", bufs=4)
             nc.sync.dma_start(out=v_of[u][:], in_=v[u // SLABS, :, slab_cols(u)])
 
         def load_g2(s):
@@ -153,29 +153,36 @@ def tile_full_tmix_params_pc_k_kernel(
         def r_times_k(j):
             u, o = j // SLAB_PASSES, j % SLAB_PASSES
             cols = slice(PASS * o, PASS * (o + 1))
-            rk_of[j] = work.tile([P, PASS], F32, name="rk", bufs=3)
+            rk_of[j] = work.tile([P, PASS], F32, name="rk", bufs=4)
             nc.gpsimd.tensor_tensor(out=rk_of[j][:], in0=r_of[u][:, cols], in1=k_of[u][:, cols], op=ALU.mult)
 
         def rk_transpose(j):
-            rk_ch_of[j] = ps_one.tile([P, BANK_BLOCKS, P], F32, name="rk_ch", tag="blocks")
+            rk_ch_of[j] = ps_rk.tile([P, BANK_BLOCKS, P], F32, name="rk_ch", tag="rk_ch")
             for i in range(BANK_BLOCKS):
                 nc.tensor.transpose(rk_ch_of[j][:, i, :], rk_of[j][:, P * i : P * (i + 1)], ident_f[:])
 
-        def rk_copy(j):
-            rk_sb_of[j] = work.tile([P, BANK_BLOCKS, P], F32, name="rk_sb", bufs=3)
-            nc.scalar.copy(out=rk_sb_of[j][:], in_=rk_ch_of[j][:])
+        def rk_high(j):
+            high_of[j] = work.tile([P, BANK_BLOCKS, P], BF16, name="rk_high", bufs=3)
+            nc.scalar.copy(out=high_of[j][:], in_=rk_ch_of[j][:])
+
+        def rk_low(j):
+            low_of[j] = work.tile([P, BANK_BLOCKS, P], BF16, name="rk_low", bufs=3)
+            nc.vector.tensor_tensor(
+                out=low_of[j][:], in0=rk_ch_of[j][:], in1=high_of[j][:], op=ALU.subtract
+            )
 
         def dot_matmul(j):
             g = j % PASSES
             dot_ps_of[j] = ps_one.tile([P, PASS_HEADS], F32, name="dot_ps")
             for i in range(BANK_BLOCKS):
-                nc.tensor.matmul(
-                    out=dot_ps_of[j][:, BLOCK_HEADS * i : BLOCK_HEADS * (i + 1)],
-                    lhsT=rk_sb_of[j][:, i, :],
-                    rhs=head_w[:, BANK_BLOCKS * g + i, :],
-                    start=True,
-                    stop=True,
-                )
+                for part in (high_of[j], low_of[j]):
+                    nc.tensor.matmul(
+                        out=dot_ps_of[j][:, BLOCK_HEADS * i : BLOCK_HEADS * (i + 1)],
+                        lhsT=part[:, i, :],
+                        rhs=head_w[:, BANK_BLOCKS * g + i, :],
+                        start=(part is high_of[j]),
+                        stop=(part is low_of[j]),
+                    )
 
         def dot_copy(j):
             dot_of[j] = stats.tile([P, PASS_HEADS], F32, name="dot", bufs=3)
@@ -221,7 +228,7 @@ def tile_full_tmix_params_pc_k_kernel(
 
         def normalise(j):
             u = j // SLAB_PASSES
-            a_tok_of[j] = work.tile([P, PACK, P], F32, name="a_tok", bufs=3)
+            a_tok_of[j] = work.tile([P, PACK, P], F32, name="a_tok", bufs=4)
             for hh, h in enumerate(step_heads(j)):
                 nc.scalar.activation(
                     out=a_tok_of[j][:, :, HEAD_PARTS * hh : HEAD_PARTS * (hh + 1)],
@@ -232,7 +239,7 @@ def tile_full_tmix_params_pc_k_kernel(
                 )
 
         def a_transpose(j):
-            a_ch_of[j] = ps_a.tile([P, PACK, P], F32, name="a_ch")
+            a_ch_of[j] = ps_one.tile([P, PACK, P], F32, name="a_ch")
             for t in range(PACK):
                 nc.tensor.transpose(a_ch_of[j][:, t, :], a_tok_of[j][:, t, :], ident_f[:])
 
@@ -285,20 +292,22 @@ def tile_full_tmix_params_pc_k_kernel(
             y2_of[j] = work.tile([P, PACK, P], F32, name="y2")
             nc.vector.tensor_tensor(out=y2_of[j][:], in0=yn_of[j][:], in1=dv_ch_of[j][:], op=ALU.add)
 
-        def gated_and_quantised(j):
-            words_of[j] = work.tile([P, P], U32, name="z_words", align_bytes=64, bufs=7)
-            scales_of[j] = work.tile([P, P], U8, name="z_scales", align_bytes=64, bufs=7)
-            z_bf = work.tile([P, P, PACK], BF16, name="z_bf", align_bytes=64)
+        def gated(j):
+            z_of[j] = work.tile([P, P, PACK], BF16, name="z_bf", align_bytes=64, bufs=3)
             nc.vector.tensor_tensor(
-                out=z_bf[:],
+                out=z_of[j][:],
                 in0=y2_of[j][:].rearrange("p t n -> p n t"),
                 in1=gate_of[j][:].rearrange("p t n -> p n t"),
                 op=ALU.mult,
             )
+
+        def quantised(j):
+            words_of[j] = work.tile([P, P], U32, name="z_words", align_bytes=64, bufs=7)
+            scales_of[j] = work.tile([P, P], U8, name="z_scales", align_bytes=64, bufs=7)
             nc.vector.quantize_mx(
                 out=words_of[j][:].bitcast(FP8X4),
                 scales=scales_of[j][:],
-                in_=z_bf[:].rearrange("p n t -> p (n t)"),
+                in_=z_of[j][:].rearrange("p n t -> p (n t)"),
             )
 
         def project(j):
@@ -335,8 +344,8 @@ def tile_full_tmix_params_pc_k_kernel(
             first = tick + lead
             return [first // SLAB_PASSES] if first % SLAB_PASSES == 0 and 0 <= first < SLAB_PASSES * slabs else []
 
-        for tick in range(-12, STEPS + 5):
-            for u in slab_due(tick, 12, SEQS * SLABS):
+        for tick in range(-13, STEPS + 5):
+            for u in slab_due(tick, 13, SEQS * SLABS):
                 load_y_r_k(u)
             for s in slab_due(tick, 8, SLABS):
                 load_g2(s)
@@ -345,46 +354,50 @@ def tile_full_tmix_params_pc_k_kernel(
             for s in slab_due(tick, 4, SLABS):
                 load_w(s)
 
-            for j in step_due(tick, 0):
-                add_bonus(j)
-            for j in step_due(tick, 3):
-                dot_copy(j)
             for u in slab_due(tick, 4, SEQS * SLABS):
                 scale_and_shift(u)
-            for j in step_due(tick, 8):
-                y_stats(j)
-            for u in slab_due(tick, 5, SEQS * SLABS):
-                variance(u)
+            for j in step_due(tick, 2):
+                dot_copy(j)
             for j in step_due(tick, 0):
-                gated_and_quantised(j)
+                add_bonus(j)
+            for j in step_due(tick, 4):
+                rk_low(j)
+            for j in step_due(tick, -1):
+                quantised(j)
+            for j in step_due(tick, 9):
+                y_stats(j)
+            for j in step_due(tick, 0):
+                gated(j)
+            for u in slab_due(tick, 6, SEQS * SLABS):
+                variance(u)
 
+            for j in step_due(tick, 5):
+                rk_high(j)
             for j in step_due(tick, 1):
                 gain_and_bias(j)
             for b in range(SEQS):
                 if tick == PASSES * (b + 1) + 4:
                     store(b)
-            for j in step_due(tick, 5):
-                rk_copy(j)
             for u in slab_due(tick, 5, SEQS * SLABS):
                 root(u)
             for j in step_due(tick, 4):
                 normalise(j)
 
-            for j in step_due(tick, 2):
-                a_transpose(j)
             for j in step_due(tick, 1):
                 dv_transpose(j)
-            for j in step_due(tick, 4):
+            for j in step_due(tick, 3):
                 dot_matmul(j)
+            for j in step_due(tick, 6):
+                rk_transpose(j)
+            for j in step_due(tick, 1):
+                gate_matmul(j)
+            for j in step_due(tick, 2):
+                a_transpose(j)
             for j in range(STEPS):
                 if j + projection_lag(j) == tick:
                     project(j)
-            for j in step_due(tick, 1):
-                gate_matmul(j)
-            for j in step_due(tick, 6):
-                rk_transpose(j)
 
+            for j in step_due(tick, 2):
+                dot_times_v(j)
             for j in step_due(tick, 8):
                 r_times_k(j)
-            for j in step_due(tick, 3):
-                dot_times_v(j)

@@ -83,22 +83,31 @@ def tile_full_tmix_params_pc_k_kernel(
         gh_t = const.tile([P, KD, SEQS, P], BF16, name="gh_t")
         nc.vector.tensor_copy(out=gh_t[:], in_=gh_ps[:])
 
-        gam_raw = const.tile([P, PASSES, PACK], BF16, name="gam_raw")
-        bet_raw = const.tile([P, PASSES, PACK], BF16, name="bet_raw")
-        nc.scalar.dma_start(out=gam_raw[:], in_=ln_g.rearrange("(g p t) -> p g t", p=P, t=PACK))
-        nc.scalar.dma_start(out=bet_raw[:], in_=ln_b.rearrange("(g p t) -> p g t", p=P, t=PACK))
+        ln_rows = const.tile([P, PASS], BF16, name="ln_rows")
+        nc.gpsimd.memset(ln_rows[:], 0.0)
+        nc.scalar.dma_start(out=ln_rows[0:PASSES, :], in_=ln_g.rearrange("(g c) -> g c", g=PASSES))
+        nc.scalar.dma_start(out=ln_rows[PASSES : 2 * PASSES, :], in_=ln_b.rearrange("(g c) -> g c", g=PASSES))
+        ln_cols = ps_rk.tile([P, PACK, P], BF16, name="ln_cols", tag="rk_ch")
+        for t in range(PACK):
+            nc.tensor.transpose(ln_cols[:, t, :], ln_rows[:, t:PASS:PACK], ident_b[:])
         gam = const.tile([P, PASSES * PACK], F32, name="gam")
         bet = const.tile([P, PASSES * PACK], F32, name="bet")
-        nc.scalar.copy(out=gam[:], in_=gam_raw[:].rearrange("p g t -> p (g t)"))
-        nc.scalar.copy(out=bet[:], in_=bet_raw[:].rearrange("p g t -> p (g t)"))
+        for first_row, cols in ((0, gam), (PASSES, bet)):
+            nc.scalar.copy(
+                out=cols[:].rearrange("p (g t) -> p g t", t=PACK),
+                in_=ln_cols[:, :, first_row : first_row + PASSES].rearrange("p t g -> p g t"),
+            )
 
         w_words = [
             const.tile([P, SLAB_PASSES, CO], U32, name="w_words%d" % s, align_bytes=64)
             for s in range(SLABS)
         ]
-        g2_rows = [const.tile([P, KD, SLAB], BF16, name="g2_rows%d" % s) for s in range(SLABS)]
+        g2_pairs = [
+            const.tile([P, KD, SLAB_PASSES, PACK // 2, P, 2], BF16, name="g2_pairs%d" % s)
+            for s in range(SLABS)
+        ]
 
-        y_of, r_of, k_of, v_of = {}, {}, {}, {}
+        y_of, r_of, k_of, v_of, g2_raw_of = {}, {}, {}, {}, {}
         bn_of, var_of, std_of, rstd_of, shift_of = {}, {}, {}, {}, {}
         z_of, words_of, scales_of, acc_of = {}, {}, {}, {}
         rk_of, rk_ch_of, high_of, low_of, dot_ps_of, dot_of = {}, {}, {}, {}, {}, {}
@@ -134,8 +143,9 @@ def tile_full_tmix_params_pc_k_kernel(
             nc.sync.dma_start(out=v_of[u][:], in_=v[u // SLABS, :, slab_cols(u)])
 
         def load_g2(s):
+            g2_raw_of[s] = loads.tile([P, KD, SLAB], BF16, name="g2_raw")
             nc.sync.dma_start(
-                out=g2_rows[s][:], in_=g2.rearrange("(kd d) c -> d kd c", kd=KD)[:, :, slab_cols(s)]
+                out=g2_raw_of[s][:], in_=g2.rearrange("(kd d) c -> d kd c", kd=KD)[:, :, slab_cols(s)]
             )
 
         def load_w(s):
@@ -148,6 +158,15 @@ def tile_full_tmix_params_pc_k_kernel(
             nc.sync.dma_start(
                 out=w_words[s][:].bitcast(I32),
                 in_=W_o_words[passes].rearrange("g p n t -> p g (n t)").bitcast(I32),
+            )
+
+        def pair_g2(j):
+            s, o = j // SLAB_PASSES, j % SLAB_PASSES
+            nc.scalar.copy(
+                out=g2_pairs[s][:, :, o].rearrange("d k u p e -> d k u (p e)").bitcast(F32),
+                in_=g2_raw_of[s][:, :, PASS * o : PASS * (o + 1)]
+                .bitcast(F32)
+                .rearrange("d k (p u) -> d k u p", u=PACK // 2),
             )
 
         def r_times_k(j):
@@ -282,7 +301,7 @@ def tile_full_tmix_params_pc_k_kernel(
                 for kd in range(KD):
                     nc.tensor.matmul(
                         out=gate_of[j][:, t, :],
-                        lhsT=g2_rows[s][:, kd, PASS * o + t : PASS * (o + 1) : PACK],
+                        lhsT=g2_pairs[s][:, kd, o, t // 2, :, t % 2],
                         rhs=gh_t[:, kd, b, :],
                         start=(kd == 0),
                         stop=(kd == KD - 1),
@@ -354,27 +373,30 @@ def tile_full_tmix_params_pc_k_kernel(
             for s in slab_due(tick, 4, SLABS):
                 load_w(s)
 
-            for u in slab_due(tick, 4, SEQS * SLABS):
-                scale_and_shift(u)
             for j in step_due(tick, 2):
                 dot_copy(j)
             for j in step_due(tick, 0):
                 add_bonus(j)
             for j in step_due(tick, 4):
                 rk_low(j)
-            for j in step_due(tick, -1):
-                quantised(j)
+            for j in step_due(tick, 0):
+                gated(j)
+            for u in slab_due(tick, 4, SEQS * SLABS):
+                scale_and_shift(u)
             for j in step_due(tick, 9):
                 y_stats(j)
             for j in step_due(tick, 0):
-                gated(j)
+                quantised(j)
             for u in slab_due(tick, 6, SEQS * SLABS):
                 variance(u)
 
-            for j in step_due(tick, 5):
-                rk_high(j)
             for j in step_due(tick, 1):
                 gain_and_bias(j)
+            for j in step_due(tick, 5):
+                rk_high(j)
+            for j in step_due(tick, 4):
+                if j < PASSES:
+                    pair_g2(j)
             for b in range(SEQS):
                 if tick == PASSES * (b + 1) + 4:
                     store(b)
@@ -387,17 +409,17 @@ def tile_full_tmix_params_pc_k_kernel(
                 dv_transpose(j)
             for j in step_due(tick, 3):
                 dot_matmul(j)
-            for j in step_due(tick, 6):
-                rk_transpose(j)
-            for j in step_due(tick, 1):
-                gate_matmul(j)
             for j in step_due(tick, 2):
                 a_transpose(j)
+            for j in step_due(tick, 1):
+                gate_matmul(j)
+            for j in step_due(tick, 6):
+                rk_transpose(j)
             for j in range(STEPS):
                 if j + projection_lag(j) == tick:
                     project(j)
 
-            for j in step_due(tick, 2):
-                dot_times_v(j)
             for j in step_due(tick, 8):
                 r_times_k(j)
+            for j in step_due(tick, 2):
+                dot_times_v(j)

@@ -53,50 +53,53 @@ def tile_full_tmix_params_pc_k_kernel(
         ps_one = ctx.enter_context(tc.psum_pool(name="ps_one", bufs=1))
         ctx.enter_context(tc.manual_schedule())
 
-        ident_f = const.tile([P, P], F32, name="ident_f")
-        make_identity(nc, ident_f[:])
-        ident_b = const.tile([P, P], BF16, name="ident_b")
-        make_identity(nc, ident_b[:])
-
-        planes = const.tile([P, SLABS, CO], U8, name="planes", align_bytes=64)
-        nc.vector.memset(planes[:].bitcast(I32), 0)
-
         rk_rows = const.tile([P, P], BF16, name="rk_rows")
         nc.vector.memset(rk_rows[:], 0.0)
+        ln_rows = const.tile([P, PASS], BF16, name="ln_rows")
+        nc.vector.memset(ln_rows[:], 0.0)
+        gh = const.tile([P, SEQS, DG], BF16, name="gh")
         nc.scalar.dma_start(
             out=rk_rows[0 : C // P, :], in_=r_k.rearrange("(j i) c -> j (i c)", i=BLOCK_HEADS)
         )
-        gh = const.tile([P, SEQS, DG], BF16, name="gh")
         nc.scalar.dma_start(out=gh[:], in_=g_hid.rearrange("b n d -> n b d"))
-        rk_cols = ps_rk.tile([P, P], BF16, name="rk_cols", tag="rk_ch")
+        nc.scalar.dma_start(out=ln_rows[0:PASSES, :], in_=ln_g.rearrange("(g c) -> g c", g=PASSES))
+        nc.scalar.dma_start(out=ln_rows[PASSES : 2 * PASSES, :], in_=ln_b.rearrange("(g c) -> g c", g=PASSES))
+
+        ident_b = const.tile([P, P], BF16, name="ident_b")
+        make_identity(nc, ident_b[:])
+        ident_f = const.tile([P, P], F32, name="ident_f")
+        make_identity(nc, ident_f[:])
+
+        rk_cols = ps_one.tile([P, P], BF16, name="rk_cols", tag="a_ch")
         nc.tensor.transpose(rk_cols[:], rk_rows[:], ident_b[:])
         head_w = const.tile([P, C // P, BLOCK_HEADS], BF16, name="head_w")
         nc.vector.memset(head_w[:], 0.0)
         for i in range(BLOCK_HEADS):
             rows = slice(HEAD * i, HEAD * (i + 1))
-            nc.vector.tensor_copy(out=head_w[rows, :, i], in_=rk_cols[rows, 0 : C // P])
+            nc.scalar.copy(out=head_w[rows, :, i], in_=rk_cols[rows, 0 : C // P])
 
-        gh_ps = ps_rk.tile([P, KD, SEQS, P], BF16, name="gh_ps", tag="rk_ch")
+        gh_ps = ps_one.tile([P, KD, SEQS, P], BF16, name="gh_ps", tag="dv_ch")
         for kd in range(KD):
             for b in range(SEQS):
                 nc.tensor.transpose(gh_ps[:, kd, b, :], gh[:, b, P * kd : P * (kd + 1)], ident_b[:])
         gh_t = const.tile([P, KD, SEQS, P], BF16, name="gh_t")
-        nc.vector.tensor_copy(out=gh_t[:], in_=gh_ps[:])
+        nc.scalar.copy(out=gh_t[:], in_=gh_ps[:])
 
-        ln_rows = const.tile([P, PASS], BF16, name="ln_rows")
-        nc.gpsimd.memset(ln_rows[:], 0.0)
-        nc.scalar.dma_start(out=ln_rows[0:PASSES, :], in_=ln_g.rearrange("(g c) -> g c", g=PASSES))
-        nc.scalar.dma_start(out=ln_rows[PASSES : 2 * PASSES, :], in_=ln_b.rearrange("(g c) -> g c", g=PASSES))
-        ln_cols = ps_rk.tile([P, PACK, P], BF16, name="ln_cols", tag="rk_ch")
-        for t in range(PACK):
-            nc.tensor.transpose(ln_cols[:, t, :], ln_rows[:, t:PASS:PACK], ident_b[:])
+        planes = const.tile([P, SLABS, CO], U8, name="planes", align_bytes=64)
+        nc.vector.memset(planes[:].bitcast(I32), 0)
+
         gam = const.tile([P, PASSES * PACK], F32, name="gam")
         bet = const.tile([P, PASSES * PACK], F32, name="bet")
-        for first_row, cols in ((0, gam), (PASSES, bet)):
-            nc.scalar.copy(
-                out=cols[:].rearrange("p (g t) -> p g t", t=PACK),
-                in_=ln_cols[:, :, first_row : first_row + PASSES].rearrange("p t g -> p g t"),
-            )
+
+        def gains_and_biases():
+            ln_cols = ps_one.tile([P, PACK, P], BF16, name="ln_cols", tag="gate")
+            for t in range(PACK):
+                nc.tensor.transpose(ln_cols[:, t, :], ln_rows[:, t:PASS:PACK], ident_b[:])
+            for first_row, cols in ((0, gam), (PASSES, bet)):
+                nc.scalar.copy(
+                    out=cols[:].rearrange("p (g t) -> p g t", t=PACK),
+                    in_=ln_cols[:, :, first_row : first_row + PASSES].rearrange("p t g -> p g t"),
+                )
 
         w_words = [
             const.tile([P, SLAB_PASSES, CO], U32, name="w_words%d" % s, align_bytes=64)
@@ -134,9 +137,12 @@ def tile_full_tmix_params_pc_k_kernel(
             for piece in range(pieces):
                 in_tile = slice(width * piece, width * (piece + 1))
                 in_hbm = slice(SLAB * (u % SLABS) + width * piece, SLAB * (u % SLABS) + width * (piece + 1))
+                if u > 0:
+                    nc.sync.dma_start(out=y_of[u][:, in_tile], in_=y[b, :, in_hbm])
                 nc.sync.dma_start(out=r_of[u][:, in_tile], in_=r[b, :, in_hbm])
                 nc.sync.dma_start(out=k_of[u][:, in_tile], in_=k[b, :, in_hbm])
-                nc.sync.dma_start(out=y_of[u][:, in_tile], in_=y[b, :, in_hbm])
+                if u == 0:
+                    nc.sync.dma_start(out=y_of[u][:, in_tile], in_=y[b, :, in_hbm])
 
         def load_v(u):
             v_of[u] = loads.tile([P, SLAB], BF16, name="v_t", bufs=4)
@@ -232,9 +238,11 @@ def tile_full_tmix_params_pc_k_kernel(
             std_of[u] = stats.tile([P, SLAB_HEADS], F32, name="std")
             nc.scalar.activation(out=std_of[u][:], in_=var_of[u][:], func=ACT.Sqrt)
 
-        def scale_and_shift(u):
+        def scale(u):
             rstd_of[u] = stats.tile([P, SLAB_HEADS], F32, name="rstd")
             nc.vector.reciprocal(out=rstd_of[u][:], in_=std_of[u][:])
+
+        def shift(u):
             shift_of[u] = stats.tile([P, SLAB_HEADS], F32, name="shift")
             nc.vector.scalar_tensor_tensor(
                 out=shift_of[u][:],
@@ -352,7 +360,10 @@ def tile_full_tmix_params_pc_k_kernel(
         def store(b):
             for half in range(HALVES):
                 res = work.tile([P, N_TILE], F32, name="res")
-                nc.scalar.copy(out=res[:], in_=acc_of[b][half][:])
+                if b == SEQS - 1 and half == HALVES - 1:
+                    nc.vector.tensor_copy(out=res[:], in_=acc_of[b][half][:])
+                else:
+                    nc.scalar.copy(out=res[:], in_=acc_of[b][half][:])
                 nc.sync.dma_start(out=out[b, :, N_TILE * half : N_TILE * (half + 1)], in_=res[:])
 
         def step_due(tick, lead):
@@ -375,51 +386,56 @@ def tile_full_tmix_params_pc_k_kernel(
 
             for j in step_due(tick, 2):
                 dot_copy(j)
+            for j in step_due(tick, -1):
+                quantised(j)
+            for u in slab_due(tick, 4, SEQS * SLABS):
+                shift(u)
             for j in step_due(tick, 0):
                 add_bonus(j)
             for j in step_due(tick, 4):
                 rk_low(j)
             for j in step_due(tick, 0):
                 gated(j)
-            for u in slab_due(tick, 4, SEQS * SLABS):
-                scale_and_shift(u)
-            for j in step_due(tick, 9):
+            for u in slab_due(tick, 5, SEQS * SLABS):
+                scale(u)
+            for j in step_due(tick, 10):
                 y_stats(j)
-            for j in step_due(tick, 0):
-                quantised(j)
-            for u in slab_due(tick, 6, SEQS * SLABS):
+            for u in slab_due(tick, 7, SEQS * SLABS):
                 variance(u)
 
+            for u in slab_due(tick, 6, SEQS * SLABS):
+                root(u)
             for j in step_due(tick, 1):
                 gain_and_bias(j)
             for j in step_due(tick, 5):
                 rk_high(j)
-            for j in step_due(tick, 4):
-                if j < PASSES:
-                    pair_g2(j)
             for b in range(SEQS):
                 if tick == PASSES * (b + 1) + 4:
                     store(b)
-            for u in slab_due(tick, 5, SEQS * SLABS):
-                root(u)
-            for j in step_due(tick, 4):
+            for j in step_due(tick, 3):
                 normalise(j)
+            for j in step_due(tick, 4):
+                if j < PASSES:
+                    pair_g2(j)
 
             for j in step_due(tick, 1):
                 dv_transpose(j)
             for j in step_due(tick, 3):
                 dot_matmul(j)
-            for j in step_due(tick, 2):
-                a_transpose(j)
-            for j in step_due(tick, 1):
-                gate_matmul(j)
             for j in step_due(tick, 6):
                 rk_transpose(j)
+            for j in step_due(tick, 1):
+                gate_matmul(j)
+            for j in step_due(tick, 2):
+                a_transpose(j)
             for j in range(STEPS):
                 if j + projection_lag(j) == tick:
                     project(j)
 
-            for j in step_due(tick, 8):
-                r_times_k(j)
+            if tick == -3:
+                gains_and_biases()
+
             for j in step_due(tick, 2):
                 dot_times_v(j)
+            for j in step_due(tick, 7):
+                r_times_k(j)

from contextlib import ExitStack

import concourse.mybir as mybir
from concourse.masks import make_identity

F32 = mybir.dt.float32
BF16 = mybir.dt.bfloat16
I32 = mybir.dt.int32
U32 = mybir.dt.uint32
U8 = mybir.dt.uint8
FP8X4 = mybir.dt.float8_e4m3fn_x4
ALU = mybir.AluOpType
ACT = mybir.ActivationFunctionType
AX = mybir.AxisListType

P = 128
SEQS = 2
C = 8192
CO = 1024
HEAD = 64
DG = 256
EPS = 0.00064
PACK = 4
PASS = P * PACK
PASSES = C // PASS
PASS_HEADS = PASS // HEAD
HEAD_PARTS = HEAD // PACK
SLAB_PASSES = 4
SLAB = SLAB_PASSES * PASS
SLABS = C // SLAB
SLAB_HEADS = SLAB // HEAD
BLOCK_HEADS = P // HEAD
BANK_BLOCKS = 4
N_TILE = 512
HALVES = CO // N_TILE
KD = DG // P
STEPS = SEQS * PASSES

FLOPS = 2 * SEQS * P * C * CO + 2 * SEQS * P * DG * C


def tile_full_tmix_params_pc_k_kernel(
    tc, y, r, k, v, g_hid, g2, r_k, ln_g, ln_b, W_o_words, W_o_scales, out
):
    nc = tc.nc
    with ExitStack() as ctx:
        const = ctx.enter_context(tc.tile_pool(name="const", bufs=1))
        loads = ctx.enter_context(tc.tile_pool(name="loads", bufs=2))
        stats = ctx.enter_context(tc.tile_pool(name="stats", bufs=2))
        work = ctx.enter_context(tc.tile_pool(name="work", bufs=2))
        ps_acc = ctx.enter_context(tc.psum_pool(name="ps_acc", bufs=1))
        ps_rk = ctx.enter_context(tc.psum_pool(name="ps_rk", bufs=2))
        ps_one = ctx.enter_context(tc.psum_pool(name="ps_one", bufs=1))
        ctx.enter_context(tc.manual_schedule())

        rk_rows = const.tile([P, P], BF16, name="rk_rows")
        nc.vector.memset(rk_rows[:], 0.0)
        ln_rows = const.tile([P, PASS], BF16, name="ln_rows")
        nc.vector.memset(ln_rows[:], 0.0)
        gh = const.tile([P, SEQS, DG], BF16, name="gh")
        nc.scalar.dma_start(
            out=rk_rows[0 : C // P, :], in_=r_k.rearrange("(j i) c -> j (i c)", i=BLOCK_HEADS)
        )
        nc.scalar.dma_start(out=gh[:], in_=g_hid.rearrange("b n d -> n b d"))
        nc.scalar.dma_start(out=ln_rows[0:PASSES, :], in_=ln_g.rearrange("(g c) -> g c", g=PASSES))
        nc.scalar.dma_start(out=ln_rows[PASSES : 2 * PASSES, :], in_=ln_b.rearrange("(g c) -> g c", g=PASSES))

        ident_b = const.tile([P, P], BF16, name="ident_b")
        make_identity(nc, ident_b[:])
        ident_f = const.tile([P, P], F32, name="ident_f")
        make_identity(nc, ident_f[:])

        rk_cols = ps_one.tile([P, P], BF16, name="rk_cols", tag="a_ch")
        nc.tensor.transpose(rk_cols[:], rk_rows[:], ident_b[:])
        head_w = const.tile([P, C // P, BLOCK_HEADS], BF16, name="head_w")
        nc.vector.memset(head_w[:], 0.0)
        for i in range(BLOCK_HEADS):
            rows = slice(HEAD * i, HEAD * (i + 1))
            nc.scalar.copy(out=head_w[rows, :, i], in_=rk_cols[rows, 0 : C // P])

        gh_ps = ps_one.tile([P, KD, SEQS, P], BF16, name="gh_ps", tag="dv_ch")
        for kd in range(KD):
            for b in range(SEQS):
                nc.tensor.transpose(gh_ps[:, kd, b, :], gh[:, b, P * kd : P * (kd + 1)], ident_b[:])
        gh_t = const.tile([P, KD, SEQS, P], BF16, name="gh_t")
        nc.scalar.copy(out=gh_t[:], in_=gh_ps[:])

        planes = const.tile([P, SLABS, CO], U8, name="planes", align_bytes=64)
        nc.vector.memset(planes[:].bitcast(I32), 0)

        gam = const.tile([P, PASSES * PACK], F32, name="gam")
        bet = const.tile([P, PASSES * PACK], F32, name="bet")

        def gains_and_biases():
            ln_cols = ps_one.tile([P, PACK, P], BF16, name="ln_cols", tag="gate")
            for t in range(PACK):
                nc.tensor.transpose(ln_cols[:, t, :], ln_rows[:, t:PASS:PACK], ident_b[:])
            for first_row, cols in ((0, gam), (PASSES, bet)):
                nc.scalar.copy(
                    out=cols[:].rearrange("p (g t) -> p g t", t=PACK),
                    in_=ln_cols[:, :, first_row : first_row + PASSES].rearrange("p t g -> p g t"),
                )

        w_words = [
            const.tile([P, SLAB_PASSES, CO], U32, name="w_words%d" % s, align_bytes=64)
            for s in range(SLABS)
        ]
        g2_pairs = [
            const.tile([P, KD, SLAB_PASSES, PACK // 2, P, 2], BF16, name="g2_pairs%d" % s)
            for s in range(SLABS)
        ]

        y_of, r_of, k_of, v_of, g2_raw_of = {}, {}, {}, {}, {}
        bn_of, var_of, std_of, rstd_of, shift_of = {}, {}, {}, {}, {}
        z_of, words_of, scales_of, acc_of = {}, {}, {}, {}
        rk_of, rk_ch_of, high_of, low_of, dot_ps_of, dot_of = {}, {}, {}, {}, {}, {}
        a_tok_of, a_ch_of, yn_of, dv_tok_of, dv_ch_of, y2_of, gate_of = {}, {}, {}, {}, {}, {}, {}

        def slab_cols(u):
            s = u % SLABS
            return slice(SLAB * s, SLAB * (s + 1))

        def step_heads(j):
            o = j % SLAB_PASSES
            return range(PASS_HEADS * o, PASS_HEADS * (o + 1))

        def by_value(head_cols):
            return head_cols.rearrange("n (p t) -> n t p", t=PACK)

        def load_y_r_k(u):
            b = u // SLABS
            y_of[u] = loads.tile([P, SLAB], BF16, name="y_t", bufs=4)
            r_of[u] = loads.tile([P, SLAB], BF16, name="r_t", bufs=4)
            k_of[u] = loads.tile([P, SLAB], BF16, name="k_t", bufs=4)
            pieces = SLAB_PASSES if u == 0 else 1
            width = SLAB // pieces
            for piece in range(pieces):
                in_tile = slice(width * piece, width * (piece + 1))
                in_hbm = slice(SLAB * (u % SLABS) + width * piece, SLAB * (u % SLABS) + width * (piece + 1))
                if u > 0:
                    nc.sync.dma_start(out=y_of[u][:, in_tile], in_=y[b, :, in_hbm])
                nc.sync.dma_start(out=r_of[u][:, in_tile], in_=r[b, :, in_hbm])
                nc.sync.dma_start(out=k_of[u][:, in_tile], in_=k[b, :, in_hbm])
                if u == 0:
                    nc.sync.dma_start(out=y_of[u][:, in_tile], in_=y[b, :, in_hbm])

        def load_v(u):
            v_of[u] = loads.tile([P, SLAB], BF16, name="v_t", bufs=4)
            nc.sync.dma_start(out=v_of[u][:], in_=v[u // SLABS, :, slab_cols(u)])

        def load_g2(s):
            g2_raw_of[s] = loads.tile([P, KD, SLAB], BF16, name="g2_raw")
            nc.sync.dma_start(
                out=g2_raw_of[s][:], in_=g2.rearrange("(kd d) c -> d kd c", kd=KD)[:, :, slab_cols(s)]
            )

        def load_w(s):
            passes = slice(SLAB_PASSES * s, SLAB_PASSES * (s + 1))
            for quad in range(4):
                nc.sync.dma_start(
                    out=planes[32 * quad : 32 * quad + 16, s, :].bitcast(I32),
                    in_=W_o_scales[passes, 4 * quad : 4 * quad + 4, :].bitcast(I32),
                )
            nc.sync.dma_start(
                out=w_words[s][:].bitcast(I32),
                in_=W_o_words[passes].rearrange("g p n t -> p g (n t)").bitcast(I32),
            )

        def pair_g2(j):
            s, o = j // SLAB_PASSES, j % SLAB_PASSES
            nc.scalar.copy(
                out=g2_pairs[s][:, :, o].rearrange("d k u p e -> d k u (p e)").bitcast(F32),
                in_=g2_raw_of[s][:, :, PASS * o : PASS * (o + 1)]
                .bitcast(F32)
                .rearrange("d k (p u) -> d k u p", u=PACK // 2),
            )

        def r_times_k(j):
            u, o = j // SLAB_PASSES, j % SLAB_PASSES
            cols = slice(PASS * o, PASS * (o + 1))
            rk_of[j] = work.tile([P, PASS], F32, name="rk", bufs=4)
            nc.gpsimd.tensor_tensor(out=rk_of[j][:], in0=r_of[u][:, cols], in1=k_of[u][:, cols], op=ALU.mult)

        def rk_transpose(j):
            rk_ch_of[j] = ps_rk.tile([P, BANK_BLOCKS, P], F32, name="rk_ch", tag="rk_ch")
            for i in range(BANK_BLOCKS):
                nc.tensor.transpose(rk_ch_of[j][:, i, :], rk_of[j][:, P * i : P * (i + 1)], ident_f[:])

        def rk_high(j):
            high_of[j] = work.tile([P, BANK_BLOCKS, P], BF16, name="rk_high", bufs=3)
            nc.scalar.copy(out=high_of[j][:], in_=rk_ch_of[j][:])

        def rk_low(j):
            low_of[j] = work.tile([P, BANK_BLOCKS, P], BF16, name="rk_low", bufs=3)
            nc.vector.tensor_tensor(
                out=low_of[j][:], in0=rk_ch_of[j][:], in1=high_of[j][:], op=ALU.subtract
            )

        def dot_matmul(j):
            g = j % PASSES
            dot_ps_of[j] = ps_one.tile([P, PASS_HEADS], F32, name="dot_ps")
            for i in range(BANK_BLOCKS):
                for part in (high_of[j], low_of[j]):
                    nc.tensor.matmul(
                        out=dot_ps_of[j][:, BLOCK_HEADS * i : BLOCK_HEADS * (i + 1)],
                        lhsT=part[:, i, :],
                        rhs=head_w[:, BANK_BLOCKS * g + i, :],
                        start=(part is high_of[j]),
                        stop=(part is low_of[j]),
                    )

        def dot_copy(j):
            dot_of[j] = stats.tile([P, PASS_HEADS], F32, name="dot", bufs=3)
            nc.vector.tensor_copy(out=dot_of[j][:], in_=dot_ps_of[j][:])

        def y_stats(j):
            u = j // SLAB_PASSES
            if j % SLAB_PASSES == 0:
                bn_of[u] = stats.tile([P, SLAB_HEADS, 3], F32, name="bn")
            for h in step_heads(j)[::2]:
                nc.vector.bn_stats(
                    out=bn_of[u][:, h : h + 2, :].rearrange("n h s -> n (h s)"),
                    in_=y_of[u][:, HEAD * h : HEAD * (h + 2)].rearrange("n (h c) -> n c h", h=2),
                )

        def variance(u):
            var_of[u] = stats.tile([P, SLAB_HEADS], F32, name="var_eps")
            nc.vector.tensor_scalar(
                out=var_of[u][:],
                in0=bn_of[u][:, :, 2],
                scalar1=1.0 / HEAD,
                scalar2=EPS,
                op0=ALU.mult,
                op1=ALU.add,
            )

        def root(u):
            std_of[u] = stats.tile([P, SLAB_HEADS], F32, name="std")
            nc.scalar.activation(out=std_of[u][:], in_=var_of[u][:], func=ACT.Sqrt)

        def scale(u):
            rstd_of[u] = stats.tile([P, SLAB_HEADS], F32, name="rstd")
            nc.vector.reciprocal(out=rstd_of[u][:], in_=std_of[u][:])

        def shift(u):
            shift_of[u] = stats.tile([P, SLAB_HEADS], F32, name="shift")
            nc.vector.scalar_tensor_tensor(
                out=shift_of[u][:],
                in0=bn_of[u][:, :, 1],
                scalar=-1.0,
                in1=rstd_of[u][:],
                op0=ALU.mult,
                op1=ALU.mult,
            )

        def normalise(j):
            u = j // SLAB_PASSES
            a_tok_of[j] = work.tile([P, PACK, P], F32, name="a_tok", bufs=4)
            for hh, h in enumerate(step_heads(j)):
                nc.scalar.activation(
                    out=a_tok_of[j][:, :, HEAD_PARTS * hh : HEAD_PARTS * (hh + 1)],
                    in_=by_value(y_of[u][:, HEAD * h : HEAD * (h + 1)]),
                    func=ACT.Identity,
                    scale=rstd_of[u][:, h : h + 1],
                    bias=shift_of[u][:, h : h + 1],
                )

        def a_transpose(j):
            a_ch_of[j] = ps_one.tile([P, PACK, P], F32, name="a_ch")
            for t in range(PACK):
                nc.tensor.transpose(a_ch_of[j][:, t, :], a_tok_of[j][:, t, :], ident_f[:])

        def gain_and_bias(j):
            g = j % PASSES
            yn_of[j] = work.tile([P, PACK, P], F32, name="yn")
            for t in range(PACK):
                col = PACK * g + t
                nc.scalar.activation(
                    out=yn_of[j][:, t, :],
                    in_=a_ch_of[j][:, t, :],
                    func=ACT.Identity,
                    scale=gam[:, col : col + 1],
                    bias=bet[:, col : col + 1],
                )

        def dot_times_v(j):
            u = j // SLAB_PASSES
            dv_tok_of[j] = work.tile([P, PACK, P], F32, name="dv_tok", bufs=3)
            o = j % SLAB_PASSES
            nc.gpsimd.tensor_tensor(
                out=dv_tok_of[j][:].rearrange("n t (h p) -> n t h p", p=HEAD_PARTS),
                in0=v_of[u][:, PASS * o : PASS * (o + 1)].rearrange(
                    "n (h p t) -> n t h p", p=HEAD_PARTS, t=PACK
                ),
                in1=dot_of[j][:].unsqueeze(1).unsqueeze(3).to_broadcast([P, PACK, PASS_HEADS, HEAD_PARTS]),
                op=ALU.mult,
            )

        def dv_transpose(j):
            dv_ch_of[j] = ps_one.tile([P, PACK, P], F32, name="dv_ch")
            for t in range(PACK):
                nc.tensor.transpose(dv_ch_of[j][:, t, :], dv_tok_of[j][:, t, :], ident_f[:])

        def gate_matmul(j):
            b, g = j // PASSES, j % PASSES
            s, o = g // SLAB_PASSES, g % SLAB_PASSES
            gate_of[j] = ps_one.tile([P, PACK, P], F32, name="gate")
            for t in range(PACK):
                for kd in range(KD):
                    nc.tensor.matmul(
                        out=gate_of[j][:, t, :],
                        lhsT=g2_pairs[s][:, kd, o, t // 2, :, t % 2],
                        rhs=gh_t[:, kd, b, :],
                        start=(kd == 0),
                        stop=(kd == KD - 1),
                    )

        def add_bonus(j):
            y2_of[j] = work.tile([P, PACK, P], F32, name="y2")
            nc.vector.tensor_tensor(out=y2_of[j][:], in0=yn_of[j][:], in1=dv_ch_of[j][:], op=ALU.add)

        def gated(j):
            z_of[j] = work.tile([P, P, PACK], BF16, name="z_bf", align_bytes=64, bufs=3)
            nc.vector.tensor_tensor(
                out=z_of[j][:],
                in0=y2_of[j][:].rearrange("p t n -> p n t"),
                in1=gate_of[j][:].rearrange("p t n -> p n t"),
                op=ALU.mult,
            )

        def quantised(j):
            words_of[j] = work.tile([P, P], U32, name="z_words", align_bytes=64, bufs=7)
            scales_of[j] = work.tile([P, P], U8, name="z_scales", align_bytes=64, bufs=7)
            nc.vector.quantize_mx(
                out=words_of[j][:].bitcast(FP8X4),
                scales=scales_of[j][:],
                in_=z_of[j][:].rearrange("p n t -> p (n t)"),
            )

        def project(j):
            b, g = j // PASSES, j % PASSES
            s, o = g // SLAB_PASSES, g % SLAB_PASSES
            if g == 0:
                acc_of[b] = [ps_acc.tile([P, N_TILE], F32, name="acc%d" % half) for half in range(HALVES)]
            for half in range(HALVES):
                n_cols = slice(N_TILE * half, N_TILE * (half + 1))
                nc.tensor.matmul_mx(
                    out=acc_of[b][half][:],
                    lhsT=words_of[j][:].bitcast(FP8X4),
                    lhsT_scale=scales_of[j][:],
                    rhs=w_words[s][:, o, n_cols].bitcast(FP8X4),
                    rhs_scale=planes[4 * o : P, s, n_cols],
                    start=(g == 0),
                    stop=(g == PASSES - 1),
                )

        def projection_lag(j):
            return 4 - max(0, j // SLAB_PASSES - SLABS)

        def store(b):
            for half in range(HALVES):
                res = work.tile([P, N_TILE], F32, name="res")
                if b == SEQS - 1 and half == HALVES - 1:
                    nc.vector.tensor_copy(out=res[:], in_=acc_of[b][half][:])
                else:
                    nc.scalar.copy(out=res[:], in_=acc_of[b][half][:])
                nc.sync.dma_start(out=out[b, :, N_TILE * half : N_TILE * (half + 1)], in_=res[:])

        def step_due(tick, lead):
            j = tick + lead
            return [j] if 0 <= j < STEPS else []

        def slab_due(tick, lead, slabs):
            first = tick + lead
            return [first // SLAB_PASSES] if first % SLAB_PASSES == 0 and 0 <= first < SLAB_PASSES * slabs else []

        for tick in range(-13, STEPS + 5):
            for u in slab_due(tick, 13, SEQS * SLABS):
                load_y_r_k(u)
            for s in slab_due(tick, 8, SLABS):
                load_g2(s)
            for u in slab_due(tick, 7, SEQS * SLABS):
                load_v(u)
            for s in slab_due(tick, 4, SLABS):
                load_w(s)

            for j in step_due(tick, 2):
                dot_copy(j)
            for j in step_due(tick, -1):
                quantised(j)
            for u in slab_due(tick, 4, SEQS * SLABS):
                shift(u)
            for j in step_due(tick, 0):
                add_bonus(j)
            for j in step_due(tick, 4):
                rk_low(j)
            for j in step_due(tick, 0):
                gated(j)
            for u in slab_due(tick, 5, SEQS * SLABS):
                scale(u)
            for j in step_due(tick, 10):
                y_stats(j)
            for u in slab_due(tick, 7, SEQS * SLABS):
                variance(u)

            for u in slab_due(tick, 6, SEQS * SLABS):
                root(u)
            for j in step_due(tick, 1):
                gain_and_bias(j)
            for j in step_due(tick, 5):
                rk_high(j)
            for b in range(SEQS):
                if tick == PASSES * (b + 1) + 4:
                    store(b)
            for j in step_due(tick, 3):
                normalise(j)
            for j in step_due(tick, 4):
                if j < PASSES:
                    pair_g2(j)

            for j in step_due(tick, 1):
                dv_transpose(j)
            for j in step_due(tick, 3):
                dot_matmul(j)
            for j in step_due(tick, 6):
                rk_transpose(j)
            for j in step_due(tick, 1):
                gate_matmul(j)
            for j in step_due(tick, 2):
                a_transpose(j)
            for j in range(STEPS):
                if j + projection_lag(j) == tick:
                    project(j)

            if tick == -3:
                gains_and_biases()

            for j in step_due(tick, 2):
                dot_times_v(j)
            for j in step_due(tick, 7):
                r_times_k(j)
